import numpy as np
import ml_dtypes


def mxq(x, axis, fmt="e4m3"):
    dtype, down = {"e4m3": (ml_dtypes.float8_e4m3fn, 7), "e5m2": (ml_dtypes.float8_e5m2, 14)}[fmt]
    v = np.moveaxis(np.asarray(x, np.float32).astype(ml_dtypes.bfloat16).astype(np.float64), axis, -1)
    blocks = v.reshape(v.shape[:-1] + (-1, 32))
    amax = np.abs(blocks).max(-1, keepdims=True)
    byte = np.maximum(np.where(amax > 0, np.frexp(amax)[1] - 1 + 127, 0) - down, 1)
    scale = np.exp2(byte - 127.0)
    codes = (blocks / scale).astype(np.float32).astype(dtype).astype(np.float64)
    return np.moveaxis((codes * scale).reshape(v.shape), -1, axis)


WIDE = False


def mx_kscale(k):
    if not WIDE:
        return np.ones(k)
    levels = np.array([20, -20, 10, -10, 0])
    if k % 512:
        return np.exp2(np.random.permutation(np.resize(levels, k // 32))).repeat(32)
    a = np.empty((k // 512, 16))
    for p in range(k // 512):
        a[p, :8] = np.random.permutation(np.resize(levels, 8))
        for g in range(8):
            far = levels[np.abs(levels - a[p, g]) >= 10]
            a[p, g + 8] = far[np.random.randint(len(far))]
    return np.exp2(a.ravel()).repeat(32)


BF16 = ml_dtypes.bfloat16


def bf(x):
    return np.asarray(x, np.float32).astype(BF16)


def f64(x):
    return np.asarray(x).astype(np.float64)


B, I, O, ORDER = 2048, 512, 512, 8
LO, HI = -1.0, 1.0


def setup_inputs():
    j = np.arange(ORDER)
    binom = np.cumprod(np.concatenate(([1.0], (ORDER - j) / (j + 1.0))))
    u = mx_kscale(O)
    x = np.random.standard_normal((B, I))
    weights = np.random.standard_normal((O, I)) / u[:, None]
    coeffs = np.random.standard_normal((O, I, ORDER + 1)) * binom / (HI - LO) ** ORDER * 2.0 / np.sqrt(I)
    g = np.random.standard_normal((B, O)) * np.exp2(np.random.randint(-12, 1, (B, 1))) * 4.0 * u
    return {"x": bf(x), "weights": bf(weights), "coeffs": bf(coeffs), "grad_out": bf(g)}


def reference(x, weights, coeffs, grad_out):
    K = coeffs.shape[-1] - 1
    zoom = (HI - LO) / 2.0
    pan = (HI + LO) / 2.0
    th = np.tanh(f64(x))
    xt = th * zoom + pan
    x_a = (xt - LO)[..., None]
    x_b = (HI - xt)[..., None]
    e = np.arange(K + 1)
    dber = e * x_a ** np.maximum(e - 1, 0) * x_b ** (K - e) - (K - e) * x_a ** e * x_b ** np.maximum(K - e - 1, 0)
    dber = dber * (zoom * (1.0 - th * th))[..., None]
    wc = f64(coeffs) * f64(weights)[..., None]
    wk = wc.reshape(wc.shape[0], -1)
    G = mxq(f64(grad_out), 1, "e5m2") @ mxq(wk, 0, "e4m3")
    G = G.reshape(dber.shape)
    return (G * dber).sum(axis=-1)

@@ -1,0 +1,298 @@
+import math
+from contextlib import ExitStack
+
+import concourse.mybir as mybir
+from concourse.masks import make_identity
+
+F32 = mybir.dt.float32
+BF16 = mybir.dt.bfloat16
+U32 = mybir.dt.uint32
+U8 = mybir.dt.uint8
+E4M3_X4 = mybir.dt.float8_e4m3fn_x4
+E5M2_X4 = mybir.dt.float8_e5m2_x4
+ALU = mybir.AluOpType
+ACT = mybir.ActivationFunctionType
+
+P = 128
+PACK = 4
+TOKENS, FEATURES, OUTPUTS, ORDER = 2048, 512, 512, 8
+TERMS = ORDER + 1
+CHUNK = 512
+BLOCKS = CHUNK // P
+N_CHUNKS = TOKENS // CHUNK
+N_GROUPS = FEATURES // P
+FLAT = 3
+X_LIMIT = 8.0
+AHEAD = 2
+
+FLOPS = 2 * TOKENS * OUTPUTS * FEATURES * TERMS
+
+
+def binomial(n, k):
+    value = 1
+    for j in range(k):
+        value = value * (n - j) // (j + 1)
+    return value
+
+
+def gamma(k):
+    return 8.0 / binomial(ORDER, k)
+
+
+def tile_custombernsteinlayer_kernel(tc, x, weights, coeffs, grad_out, out):
+    nc = tc.nc
+    with ExitStack() as ctx:
+        keep = ctx.enter_context(tc.tile_pool(name="keep", bufs=1))
+        stage = ctx.enter_context(tc.tile_pool(name="stage", bufs=2))
+        mx_psum = ctx.enter_context(tc.psum_pool(name="mx_psum", bufs=5))
+        tr_psum = ctx.enter_context(tc.psum_pool(name="tr_psum", bufs=2))
+        sum_psum = ctx.enter_context(tc.psum_pool(name="sum_psum", bufs=1))
+
+        ident_f32 = keep.tile([P, P], F32)
+        make_identity(nc, ident_f32[:])
+        ident_bf16 = keep.tile([P, P], BF16)
+        make_identity(nc, ident_bf16[:])
+
+        x_rows = keep.tile([P, N_CHUNKS * BLOCKS, FEATURES], BF16)
+        g_rows = keep.tile([P, N_CHUNKS * BLOCKS, OUTPUTS], BF16)
+        w_rows = keep.tile([P, PACK, FEATURES], BF16)
+        w_words = keep.tile([P, FEATURES, PACK], BF16)
+        g_codes = keep.tile([P, TOKENS], U32, align_bytes=64)
+        g_scales = keep.tile([P, TOKENS], U8, align_bytes=64)
+        wc_codes = keep.tile([P, N_GROUPS, TERMS * P], U32, align_bytes=64)
+        wc_scales = keep.tile([P, N_GROUPS, TERMS * P], U8, align_bytes=64)
+
+        coeff_view = coeffs.rearrange("(p t) i k -> p t (i k)", t=PACK)
+        group_cols = P * TERMS
+        coeff_tiles = {}
+
+        def load_coeffs(group):
+            co = stage.tile([P, PACK, group_cols], BF16, tag="co")
+            nc.sync.dma_start(out=co[:], in_=coeff_view[:, :, group * group_cols : (group + 1) * group_cols])
+            coeff_tiles[group] = co
+
+        def load_tokens(chunk):
+            rows = slice(chunk * CHUNK, (chunk + 1) * CHUNK)
+            blocks = slice(chunk * BLOCKS, (chunk + 1) * BLOCKS)
+            nc.sync.dma_start(out=x_rows[:, blocks, :], in_=x[rows, :].rearrange("(b p) i -> p b i", p=P))
+            nc.sync.dma_start(out=g_rows[:, blocks, :], in_=grad_out[rows, :].rearrange("(b p) o -> p b o", p=P))
+
+        def quantise_wc(group):
+            wq = stage.tile([P, TERMS, P, PACK], BF16, tag="wq", bufs=1, align_bytes=64)
+            by_plane = coeff_tiles[group][:].rearrange("p t (i k) -> p k i t", k=TERMS)
+            for k in range(TERMS):
+                nc.gpsimd.tensor_scalar(
+                    out=wq[:, k, :, :], in0=by_plane[:, k, :, :], scalar1=1.0, scalar2=0.0, op0=ALU.mult, op1=ALU.add
+                )
+            if group + 2 < N_GROUPS:
+                load_coeffs(group + 2)
+            nc.vector.tensor_tensor(
+                out=wq[:],
+                in0=wq[:],
+                in1=w_words[:, group * P : (group + 1) * P, :].unsqueeze(1).to_broadcast([P, TERMS, P, PACK]),
+                op=ALU.mult,
+            )
+            flat = wq[:].rearrange("p k i t -> p (k i t)")
+            wide = ORDER * P
+            nc.vector.quantize_mx(
+                out=wc_codes[:, group, 0:wide].bitcast(E4M3_X4),
+                scales=wc_scales[:, group, 0:wide],
+                in_=flat[:, 0 : wide * PACK],
+            )
+            nc.vector.quantize_mx(
+                out=wc_codes[:, group, wide : wide + P].bitcast(E4M3_X4),
+                scales=wc_scales[:, group, wide : wide + P],
+                in_=flat[:, wide * PACK : (wide + P) * PACK],
+            )
+
+        def clamp_x(chunk):
+            blocks = slice(chunk * BLOCKS, (chunk + 1) * BLOCKS)
+            nc.vector.tensor_scalar(
+                out=x_rows[:, blocks, :], in0=x_rows[:, blocks, :],
+                scalar1=-X_LIMIT, scalar2=X_LIMIT, op0=ALU.max, op1=ALU.min,
+            )
+
+        def quantise_grad(chunk):
+            g_words = g_rows[:].bitcast(F32)
+            gq = stage.tile([P, CHUNK * PACK], BF16, tag="gq", align_bytes=64)
+            gq_words = gq[:].bitcast(F32).rearrange("p (n u) -> p n u", u=2)
+            for half in range(2):
+                g_t = tr_psum.tile([P, 2, 2 * P], F32, tag="tr")
+                for b in range(2):
+                    block = chunk * BLOCKS + 2 * half + b
+                    for u in range(2):
+                        nc.tensor.transpose(
+                            out=g_t[:, u, b * P : (b + 1) * P],
+                            in_=g_words[:, block, u : 2 * P : 2],
+                            identity=ident_f32[:],
+                        )
+                nc.scalar.copy(
+                    out=gq_words[:, half * 2 * P : (half + 1) * 2 * P, :],
+                    in_=g_t[:].rearrange("p u n -> p n u"),
+                )
+            cols = slice(chunk * CHUNK, (chunk + 1) * CHUNK)
+            nc.vector.quantize_mx(out=g_codes[:, cols].bitcast(E5M2_X4), scales=g_scales[:, cols], in_=gq[:])
+
+        def first_use(step):
+            group, chunk = step
+            if group == 0:
+                clamp_x(chunk)
+                quantise_grad(chunk)
+            if chunk == 0:
+                quantise_wc(group)
+
+        def scalar_planes(step):
+            group, chunk = step
+            x_t = tr_psum.tile([P, CHUNK], BF16, tag="tr")
+            for b in range(BLOCKS):
+                nc.tensor.transpose(
+                    out=x_t[:, b * P : (b + 1) * P],
+                    in_=x_rows[:, chunk * BLOCKS + b, group * P : (group + 1) * P],
+                    identity=ident_bf16[:],
+                )
+            e_planes = stage.tile([P, ORDER, CHUNK], F32, tag="e_planes")
+            s_planes = stage.tile([P, 2, CHUNK], F32, tag="s_planes")
+            d_planes = stage.tile([P, 3, CHUNK], F32, tag="d_planes")
+
+            def exp_plane(j, gain):
+                nc.scalar.activation(
+                    out=e_planes[:, j, :], in_=x_t[:], func=ACT.Exp, scale=float(2 * (j - FLAT)), bias=math.log(gain)
+                )
+
+            recipe = {
+                0: ("times", e_planes[:, 0, :], gamma(0)),
+                1: ("times", d_planes[:, 0, :], -gamma(1)),
+                ORDER - 2: ("times", d_planes[:, 1, :], -gamma(ORDER - 2)),
+                ORDER - 1: ("times", d_planes[:, 2, :], -gamma(ORDER - 1)),
+                ORDER: ("times", e_planes[:, ORDER - 1, :], -gamma(ORDER)),
+            }
+            exp_plane(0, binomial(ORDER - 1, 0))
+            exp_plane(1, binomial(ORDER - 1, 1))
+            flat = binomial(ORDER - 1, FLAT)
+            for side in (-1, 1):
+                near = binomial(ORDER - 1, FLAT + side)
+                far = binomial(ORDER - 1, FLAT + 2 * side)
+                k_near = FLAT if side < 0 else FLAT + 1
+                k_far = k_near + side
+                middle = near / (2.0 * far)
+                line = e_planes[:, FLAT + side, :]
+                square = s_planes[:, (side + 1) // 2, :]
+                exp_plane(FLAT + side, gamma(k_near) * near)
+                root = math.sqrt(gamma(k_far) * far)
+                nc.scalar.activation(
+                    out=square, in_=line, func=ACT.Square, scale=root / (gamma(k_near) * near), bias=-root * middle
+                )
+                for k, plane, constant in (
+                    (k_near, line, gamma(k_near) * flat),
+                    (k_far, square, gamma(k_far) * near * near / (4.0 * far)),
+                ):
+                    if side > 0:
+                        recipe[k] = ("minus", plane, constant)
+                    else:
+                        nc.scalar.activation(out=plane, in_=plane, func=ACT.Identity, scale=-1.0, bias=constant)
+                        recipe[k] = ("times", plane, 1.0)
+            for j in range(FLAT + 2, ORDER):
+                exp_plane(j, binomial(ORDER - 1, j))
+            x_part = x_rows[:, chunk * BLOCKS : (chunk + 1) * BLOCKS, group * P : (group + 1) * P]
+            t_part = stage.tile([P, BLOCKS, P], F32, tag="t_part", bufs=3)
+            c_part = stage.tile([P, BLOCKS, P], F32, tag="c_part", bufs=3)
+            nc.scalar.activation(out=t_part[:], in_=x_part, func=ACT.Tanh)
+            nc.scalar.activation(out=c_part[:], in_=t_part[:], func=ACT.Square)
+            nc.scalar.activation(out=c_part[:], in_=c_part[:], func=ACT.Square, scale=-1.0, bias=1.0)
+            nc.scalar.activation(out=c_part[:], in_=c_part[:], func=ACT.Square)
+            return {"e": e_planes, "d": d_planes, "recipe": recipe, "t": t_part, "c": c_part}
+
+        def vector_planes(made):
+            e_planes, d_planes = made["e"], made["d"]
+            nc.vector.tensor_tensor(
+                out=d_planes[:, 0, :], in0=e_planes[:, 0, :], in1=e_planes[:, 1, :], op=ALU.subtract
+            )
+            nc.vector.tensor_tensor(
+                out=d_planes[:, 1:3, :], in0=e_planes[:, ORDER - 3 : ORDER - 1, :],
+                in1=e_planes[:, ORDER - 2 : ORDER, :], op=ALU.subtract,
+            )
+
+        def multiply(step, made):
+            group, chunk = step
+            products = stage.tile([P, TERMS, CHUNK], F32, tag="products")
+            cols = slice(chunk * CHUNK, (chunk + 1) * CHUNK)
+            for k in range(TERMS):
+                g_k = mx_psum.tile([P, CHUNK], F32, tag="g_k")
+                nc.tensor.matmul_mx(
+                    out=g_k[:],
+                    lhsT=wc_codes[:, group, k * P : (k + 1) * P].bitcast(E4M3_X4),
+                    lhsT_scale=wc_scales[:, group, k * P : (k + 1) * P],
+                    rhs=g_codes[:, cols].bitcast(E5M2_X4),
+                    rhs_scale=g_scales[:, cols],
+                    start=True,
+                    stop=True,
+                )
+                form, plane, number = made["recipe"][k]
+                if form == "times":
+                    nc.vector.scalar_tensor_tensor(
+                        out=products[:, k, :], in0=g_k[:], scalar=number, in1=plane, op0=ALU.mult, op1=ALU.mult
+                    )
+                else:
+                    nc.vector.scalar_tensor_tensor(
+                        out=products[:, k, :], in0=plane, scalar=number, in1=g_k[:], op0=ALU.subtract, op1=ALU.mult
+                    )
+            return products
+
+        def sum_and_store(step, made, products):
+            group, chunk = step
+            total = sum_psum.tile([P, BLOCKS, P], F32, tag="total")
+            for b in range(BLOCKS):
+                for k in range(TERMS):
+                    nc.tensor.matmul(
+                        out=total[:, b, :],
+                        lhsT=products[:, k, b * P : (b + 1) * P],
+                        rhs=ident_f32[:],
+                        is_transpose=True,
+                        start=(k == 0),
+                        stop=(k == TERMS - 1),
+                    )
+            h_part = stage.tile([P, BLOCKS, P], F32, tag="h_part")
+            nc.vector.scalar_tensor_tensor(
+                out=h_part[:], in0=made["t"][:], scalar=1.0, in1=made["c"][:], op0=ALU.subtract, op1=ALU.mult
+            )
+            result = stage.tile([P, BLOCKS, P], F32, tag="result")
+            nc.vector.tensor_tensor(out=result[:], in0=total[:], in1=h_part[:], op=ALU.mult)
+            nc.sync.dma_start(
+                out=out[chunk * CHUNK : (chunk + 1) * CHUNK, group * P : (group + 1) * P].rearrange(
+                    "(b p) i -> p b i", p=P
+                ),
+                in_=result[:],
+            )
+
+        load_coeffs(0)
+        nc.sync.dma_start(out=w_rows[:], in_=weights.rearrange("(p t) i -> p t i", t=PACK))
+        load_tokens(0)
+        load_tokens(1)
+        load_coeffs(1)
+        load_tokens(2)
+        load_tokens(3)
+
+        steps = [(group, chunk) for group in range(N_GROUPS) for chunk in range(N_CHUNKS)]
+        made = {}
+        products = {}
+
+        clamp_x(0)
+        made[0] = scalar_planes(steps[0])
+        nc.vector.tensor_copy(out=w_words[:], in_=w_rows[:].rearrange("p t i -> p i t"))
+        quantise_wc(0)
+        quantise_grad(0)
+        vector_planes(made[0])
+        for s in range(1, AHEAD):
+            first_use(steps[s])
+
+        for s in range(len(steps) + 1):
+            if s + 1 < len(steps):
+                made[s + 1] = scalar_planes(steps[s + 1])
+            if s < len(steps):
+                products[s] = multiply(steps[s], made[s])
+            if s + 1 < len(steps):
+                vector_planes(made[s + 1])
+            if s + AHEAD < len(steps):
+                first_use(steps[s + AHEAD])
+            if s >= 1:
+                sum_and_store(steps[s - 1], made[s - 1], products[s - 1])

@@ -23,6 +23,7 @@ N_CHUNKS = TOKENS // CHUNK
 N_GROUPS = FEATURES // P
 FLAT = 3
 X_LIMIT = 8.0
+NEGATED = (FLAT - 1, FLAT)
 AHEAD = 2
 
 FLOPS = 2 * TOKENS * OUTPUTS * FEATURES * TERMS
@@ -82,7 +83,8 @@ def tile_custombernsteinlayer_kernel(tc, x, weights, coeffs, grad_out, out):
             by_plane = coeff_tiles[group][:].rearrange("p t (i k) -> p k i t", k=TERMS)
             for k in range(TERMS):
                 nc.gpsimd.tensor_scalar(
-                    out=wq[:, k, :, :], in0=by_plane[:, k, :, :], scalar1=1.0, scalar2=0.0, op0=ALU.mult, op1=ALU.add
+                    out=wq[:, k, :, :], in0=by_plane[:, k, :, :],
+                    scalar1=-1.0 if k in NEGATED else 1.0, scalar2=0.0, op0=ALU.mult, op1=ALU.add,
                 )
             if group + 2 < N_GROUPS:
                 load_coeffs(group + 2)
@@ -186,11 +188,7 @@ def tile_custombernsteinlayer_kernel(tc, x, weights, coeffs, grad_out, out):
                     (k_near, line, gamma(k_near) * flat),
                     (k_far, square, gamma(k_far) * near * near / (4.0 * far)),
                 ):
-                    if side > 0:
-                        recipe[k] = ("minus", plane, constant)
-                    else:
-                        nc.scalar.activation(out=plane, in_=plane, func=ACT.Identity, scale=-1.0, bias=constant)
-                        recipe[k] = ("times", plane, 1.0)
+                    recipe[k] = ("minus", plane, constant)
             for j in range(FLAT + 2, ORDER):
                 exp_plane(j, binomial(ORDER - 1, j))
             x_part = x_rows[:, chunk * BLOCKS : (chunk + 1) * BLOCKS, group * P : (group + 1) * P]
@@ -202,12 +200,12 @@ def tile_custombernsteinlayer_kernel(tc, x, weights, coeffs, grad_out, out):
             nc.scalar.activation(out=c_part[:], in_=c_part[:], func=ACT.Square)
             return {"e": e_planes, "d": d_planes, "recipe": recipe, "t": t_part, "c": c_part}
 
-        def vector_planes(made):
+        def difference_planes(made):
             e_planes, d_planes = made["e"], made["d"]
-            nc.vector.tensor_tensor(
+            nc.gpsimd.tensor_tensor(
                 out=d_planes[:, 0, :], in0=e_planes[:, 0, :], in1=e_planes[:, 1, :], op=ALU.subtract
             )
-            nc.vector.tensor_tensor(
+            nc.gpsimd.tensor_tensor(
                 out=d_planes[:, 1:3, :], in0=e_planes[:, ORDER - 3 : ORDER - 1, :],
                 in1=e_planes[:, ORDER - 2 : ORDER, :], op=ALU.subtract,
             )
@@ -251,12 +249,12 @@ def tile_custombernsteinlayer_kernel(tc, x, weights, coeffs, grad_out, out):
                         start=(k == 0),
                         stop=(k == TERMS - 1),
                     )
-            h_part = stage.tile([P, BLOCKS, P], F32, tag="h_part")
+            scaled = stage.tile([P, BLOCKS, P], F32, tag="scaled")
             nc.vector.scalar_tensor_tensor(
-                out=h_part[:], in0=made["t"][:], scalar=1.0, in1=made["c"][:], op0=ALU.subtract, op1=ALU.mult
+                out=scaled[:], in0=made["t"][:], scalar=1.0, in1=total[:], op0=ALU.subtract, op1=ALU.mult
             )
             result = stage.tile([P, BLOCKS, P], F32, tag="result")
-            nc.vector.tensor_tensor(out=result[:], in0=total[:], in1=h_part[:], op=ALU.mult)
+            nc.gpsimd.tensor_tensor(out=result[:], in0=scaled[:], in1=made["c"][:], op=ALU.mult)
             nc.sync.dma_start(
                 out=out[chunk * CHUNK : (chunk + 1) * CHUNK, group * P : (group + 1) * P].rearrange(
                     "(b p) i -> p b i", p=P
@@ -281,7 +279,7 @@ def tile_custombernsteinlayer_kernel(tc, x, weights, coeffs, grad_out, out):
         nc.vector.tensor_copy(out=w_words[:], in_=w_rows[:].rearrange("p t i -> p i t"))
         quantise_wc(0)
         quantise_grad(0)
-        vector_planes(made[0])
+        difference_planes(made[0])
         for s in range(1, AHEAD):
             first_use(steps[s])
 
@@ -291,7 +289,7 @@ def tile_custombernsteinlayer_kernel(tc, x, weights, coeffs, grad_out, out):
             if s < len(steps):
                 products[s] = multiply(steps[s], made[s])
             if s + 1 < len(steps):
-                vector_planes(made[s + 1])
+                difference_planes(made[s + 1])
             if s + AHEAD < len(steps):
                 first_use(steps[s + AHEAD])
             if s >= 1:

@@ -24,7 +24,9 @@ N_GROUPS = FEATURES // P
 FLAT = 3
 X_LIMIT = 8.0
 NEGATED = (FLAT - 1, FLAT)
-AHEAD = 2
+K_ORDER = (0, ORDER, FLAT, FLAT + 1, 1, FLAT - 1, FLAT + 2, ORDER - 2, ORDER - 1)
+PARTS = ((0, 2), (2, 2), (4, 2), (6, 2), (8, 1))
+EARLY = 4
 
 FLOPS = 2 * TOKENS * OUTPUTS * FEATURES * TERMS
 
@@ -55,7 +57,6 @@ def tile_custombernsteinlayer_kernel(tc, x, weights, coeffs, grad_out, out):
         make_identity(nc, ident_bf16[:])
 
         x_rows = keep.tile([P, N_CHUNKS * BLOCKS, FEATURES], BF16)
-        g_rows = keep.tile([P, N_CHUNKS * BLOCKS, OUTPUTS], BF16)
         w_rows = keep.tile([P, PACK, FEATURES], BF16)
         w_words = keep.tile([P, FEATURES, PACK], BF16)
         g_codes = keep.tile([P, TOKENS], U32, align_bytes=64)
@@ -66,45 +67,56 @@ def tile_custombernsteinlayer_kernel(tc, x, weights, coeffs, grad_out, out):
         coeff_view = coeffs.rearrange("(p t) i k -> p t (i k)", t=PACK)
         group_cols = P * TERMS
         coeff_tiles = {}
+        grad_tiles = {}
+        gq_tiles = {}
+        wq_tiles = {}
 
         def load_coeffs(group):
             co = stage.tile([P, PACK, group_cols], BF16, tag="co")
             nc.sync.dma_start(out=co[:], in_=coeff_view[:, :, group * group_cols : (group + 1) * group_cols])
             coeff_tiles[group] = co
 
-        def load_tokens(chunk):
+        def load_x(chunk):
             rows = slice(chunk * CHUNK, (chunk + 1) * CHUNK)
             blocks = slice(chunk * BLOCKS, (chunk + 1) * BLOCKS)
             nc.sync.dma_start(out=x_rows[:, blocks, :], in_=x[rows, :].rearrange("(b p) i -> p b i", p=P))
-            nc.sync.dma_start(out=g_rows[:, blocks, :], in_=grad_out[rows, :].rearrange("(b p) o -> p b o", p=P))
 
-        def quantise_wc(group):
-            wq = stage.tile([P, TERMS, P, PACK], BF16, tag="wq", bufs=1, align_bytes=64)
+        def load_grad(chunk):
+            rows = slice(chunk * CHUNK, (chunk + 1) * CHUNK)
+            g_rows = stage.tile([P, BLOCKS, OUTPUTS], BF16, tag="g_rows", bufs=4)
+            nc.sync.dma_start(out=g_rows[:], in_=grad_out[rows, :].rearrange("(b p) o -> p b o", p=P))
+            grad_tiles[chunk] = g_rows
+
+        def regroup(group, part):
+            first, count = PARTS[part]
+            wq = stage.tile([P, 2, P, PACK], BF16, tag="wq", bufs=3, align_bytes=64)
             by_plane = coeff_tiles[group][:].rearrange("p t (i k) -> p k i t", k=TERMS)
-            for k in range(TERMS):
+            for j in range(count):
+                k = K_ORDER[first + j]
                 nc.gpsimd.tensor_scalar(
-                    out=wq[:, k, :, :], in0=by_plane[:, k, :, :],
+                    out=wq[:, j, :, :], in0=by_plane[:, k, :, :],
                     scalar1=-1.0 if k in NEGATED else 1.0, scalar2=0.0, op0=ALU.mult, op1=ALU.add,
                 )
-            if group + 2 < N_GROUPS:
-                load_coeffs(group + 2)
+            wq_tiles[group, part] = wq
+
+        def multiply_wc(group, part):
+            count = PARTS[part][1]
+            wq = wq_tiles[group, part]
             nc.vector.tensor_tensor(
-                out=wq[:],
-                in0=wq[:],
-                in1=w_words[:, group * P : (group + 1) * P, :].unsqueeze(1).to_broadcast([P, TERMS, P, PACK]),
+                out=wq[:, 0:count, :, :],
+                in0=wq[:, 0:count, :, :],
+                in1=w_words[:, group * P : (group + 1) * P, :].unsqueeze(1).to_broadcast([P, count, P, PACK]),
                 op=ALU.mult,
             )
-            flat = wq[:].rearrange("p k i t -> p (k i t)")
-            wide = ORDER * P
+
+        def quantise_wc(group, part):
+            first, count = PARTS[part]
+            cols = slice(first * P, (first + count) * P)
+            flat = wq_tiles[group, part][:].rearrange("p k i t -> p (k i t)")
             nc.vector.quantize_mx(
-                out=wc_codes[:, group, 0:wide].bitcast(E4M3_X4),
-                scales=wc_scales[:, group, 0:wide],
-                in_=flat[:, 0 : wide * PACK],
-            )
-            nc.vector.quantize_mx(
-                out=wc_codes[:, group, wide : wide + P].bitcast(E4M3_X4),
-                scales=wc_scales[:, group, wide : wide + P],
-                in_=flat[:, wide * PACK : (wide + P) * PACK],
+                out=wc_codes[:, group, cols].bitcast(E4M3_X4),
+                scales=wc_scales[:, group, cols],
+                in_=flat[:, 0 : count * P * PACK],
             )
 
         def clamp_x(chunk):
@@ -114,36 +126,31 @@ def tile_custombernsteinlayer_kernel(tc, x, weights, coeffs, grad_out, out):
                 scalar1=-X_LIMIT, scalar2=X_LIMIT, op0=ALU.max, op1=ALU.min,
             )
 
+        def turn_grad(chunk, half):
+            if half == 0:
+                gq = stage.tile([P, CHUNK * PACK], BF16, tag="gq", align_bytes=64)
+                gq_tiles[chunk] = gq
+            g_words = grad_tiles[chunk][:].bitcast(F32)
+            gq_words = gq_tiles[chunk][:].bitcast(F32).rearrange("p (n u) -> p n u", u=2)
+            g_t = mx_psum.tile([P, 2, 2 * P], F32, tag="g_k")
+            for b in range(2):
+                for u in range(2):
+                    nc.tensor.transpose(
+                        out=g_t[:, u, b * P : (b + 1) * P],
+                        in_=g_words[:, 2 * half + b, u : 2 * P : 2],
+                        identity=ident_f32[:],
+                    )
+            nc.vector.tensor_copy(
+                out=gq_words[:, half * 2 * P : (half + 1) * 2 * P, :], in_=g_t[:].rearrange("p u n -> p n u")
+            )
+
         def quantise_grad(chunk):
-            g_words = g_rows[:].bitcast(F32)
-            gq = stage.tile([P, CHUNK * PACK], BF16, tag="gq", align_bytes=64)
-            gq_words = gq[:].bitcast(F32).rearrange("p (n u) -> p n u", u=2)
-            for half in range(2):
-                g_t = tr_psum.tile([P, 2, 2 * P], F32, tag="tr")
-                for b in range(2):
-                    block = chunk * BLOCKS + 2 * half + b
-                    for u in range(2):
-                        nc.tensor.transpose(
-                            out=g_t[:, u, b * P : (b + 1) * P],
-                            in_=g_words[:, block, u : 2 * P : 2],
-                            identity=ident_f32[:],
-                        )
-                nc.scalar.copy(
-                    out=gq_words[:, half * 2 * P : (half + 1) * 2 * P, :],
-                    in_=g_t[:].rearrange("p u n -> p n u"),
-                )
             cols = slice(chunk * CHUNK, (chunk + 1) * CHUNK)
-            nc.vector.quantize_mx(out=g_codes[:, cols].bitcast(E5M2_X4), scales=g_scales[:, cols], in_=gq[:])
+            nc.vector.quantize_mx(
+                out=g_codes[:, cols].bitcast(E5M2_X4), scales=g_scales[:, cols], in_=gq_tiles[chunk][:]
+            )
 
-        def first_use(step):
-            group, chunk = step
-            if group == 0:
-                clamp_x(chunk)
-                quantise_grad(chunk)
-            if chunk == 0:
-                quantise_wc(group)
-
-        def scalar_planes(step):
+        def turn_x(step):
             group, chunk = step
             x_t = tr_psum.tile([P, CHUNK], BF16, tag="tr")
             for b in range(BLOCKS):
@@ -152,109 +159,118 @@ def tile_custombernsteinlayer_kernel(tc, x, weights, coeffs, grad_out, out):
                     in_=x_rows[:, chunk * BLOCKS + b, group * P : (group + 1) * P],
                     identity=ident_bf16[:],
                 )
-            e_planes = stage.tile([P, ORDER, CHUNK], F32, tag="e_planes")
-            s_planes = stage.tile([P, 2, CHUNK], F32, tag="s_planes")
-            d_planes = stage.tile([P, 3, CHUNK], F32, tag="d_planes")
+            return x_t
 
-            def exp_plane(j, gain):
+        def scalar_planes(step, x_t):
+            group, chunk = step
+            e_low0 = stage.tile([P, CHUNK], F32, tag="e_low0")
+            e_low1 = stage.tile([P, CHUNK], F32, tag="e_low1")
+            e_high = stage.tile([P, 3, CHUNK], F32, tag="e_high")
+            line_low = stage.tile([P, CHUNK], F32, tag="line_low")
+            line_high = stage.tile([P, CHUNK], F32, tag="line_high")
+            square_low = stage.tile([P, CHUNK], F32, tag="square_low")
+            square_high = stage.tile([P, CHUNK], F32, tag="square_high")
+            d_low = stage.tile([P, CHUNK], F32, tag="d_low")
+            d_high = stage.tile([P, 2, CHUNK], F32, tag="d_high")
+            t_part = stage.tile([P, BLOCKS, P], F32, tag="t_part", bufs=3)
+            c_part = stage.tile([P, BLOCKS, P], F32, tag="c_part", bufs=3)
+            x_part = x_rows[:, chunk * BLOCKS : (chunk + 1) * BLOCKS, group * P : (group + 1) * P]
+
+            def exp_plane(out_plane, j, gain):
                 nc.scalar.activation(
-                    out=e_planes[:, j, :], in_=x_t[:], func=ACT.Exp, scale=float(2 * (j - FLAT)), bias=math.log(gain)
+                    out=out_plane, in_=x_t[:], func=ACT.Exp, scale=float(2 * (j - FLAT)), bias=math.log(gain)
                 )
 
             recipe = {
-                0: ("times", e_planes[:, 0, :], gamma(0)),
-                1: ("times", d_planes[:, 0, :], -gamma(1)),
-                ORDER - 2: ("times", d_planes[:, 1, :], -gamma(ORDER - 2)),
-                ORDER - 1: ("times", d_planes[:, 2, :], -gamma(ORDER - 1)),
-                ORDER: ("times", e_planes[:, ORDER - 1, :], -gamma(ORDER)),
+                0: ("times", e_low0[:], gamma(0)),
+                1: ("times", d_low[:], -gamma(1)),
+                ORDER - 2: ("times", d_high[:, 0, :], -gamma(ORDER - 2)),
+                ORDER - 1: ("times", d_high[:, 1, :], -gamma(ORDER - 1)),
+                ORDER: ("times", e_high[:, 2, :], -gamma(ORDER)),
             }
-            exp_plane(0, binomial(ORDER - 1, 0))
-            exp_plane(1, binomial(ORDER - 1, 1))
+            exp_plane(e_low0[:], 0, binomial(ORDER - 1, 0))
+            exp_plane(e_low1[:], 1, binomial(ORDER - 1, 1))
+            for j in range(FLAT + 2, ORDER):
+                exp_plane(e_high[:, j - FLAT - 2, :], j, binomial(ORDER - 1, j))
             flat = binomial(ORDER - 1, FLAT)
-            for side in (-1, 1):
+            squares = []
+            for side, line, square in ((-1, line_low, square_low), (1, line_high, square_high)):
                 near = binomial(ORDER - 1, FLAT + side)
                 far = binomial(ORDER - 1, FLAT + 2 * side)
                 k_near = FLAT if side < 0 else FLAT + 1
                 k_far = k_near + side
                 middle = near / (2.0 * far)
-                line = e_planes[:, FLAT + side, :]
-                square = s_planes[:, (side + 1) // 2, :]
-                exp_plane(FLAT + side, gamma(k_near) * near)
                 root = math.sqrt(gamma(k_far) * far)
-                nc.scalar.activation(
-                    out=square, in_=line, func=ACT.Square, scale=root / (gamma(k_near) * near), bias=-root * middle
-                )
-                for k, plane, constant in (
-                    (k_near, line, gamma(k_near) * flat),
-                    (k_far, square, gamma(k_far) * near * near / (4.0 * far)),
-                ):
-                    recipe[k] = ("minus", plane, constant)
-            for j in range(FLAT + 2, ORDER):
-                exp_plane(j, binomial(ORDER - 1, j))
-            x_part = x_rows[:, chunk * BLOCKS : (chunk + 1) * BLOCKS, group * P : (group + 1) * P]
-            t_part = stage.tile([P, BLOCKS, P], F32, tag="t_part", bufs=3)
-            c_part = stage.tile([P, BLOCKS, P], F32, tag="c_part", bufs=3)
+                recipe[k_near] = ("minus", line[:], gamma(k_near) * flat)
+                recipe[k_far] = ("minus", square[:], gamma(k_far) * near * near / (4.0 * far))
+                squares.append((square, line, root / (gamma(k_near) * near), -root * middle))
             nc.scalar.activation(out=t_part[:], in_=x_part, func=ACT.Tanh)
+            exp_plane(line_low[:], FLAT - 1, gamma(FLAT) * binomial(ORDER - 1, FLAT - 1))
             nc.scalar.activation(out=c_part[:], in_=t_part[:], func=ACT.Square)
+            exp_plane(line_high[:], FLAT + 1, gamma(FLAT + 1) * binomial(ORDER - 1, FLAT + 1))
             nc.scalar.activation(out=c_part[:], in_=c_part[:], func=ACT.Square, scale=-1.0, bias=1.0)
+            for square, line, scale, bias in squares[:1]:
+                nc.scalar.activation(out=square[:], in_=line[:], func=ACT.Square, scale=scale, bias=bias)
             nc.scalar.activation(out=c_part[:], in_=c_part[:], func=ACT.Square)
-            return {"e": e_planes, "d": d_planes, "recipe": recipe, "t": t_part, "c": c_part}
+            for square, line, scale, bias in squares[1:]:
+                nc.scalar.activation(out=square[:], in_=line[:], func=ACT.Square, scale=scale, bias=bias)
+            return {
+                "e_low0": e_low0, "e_low1": e_low1, "e_high": e_high, "d_low": d_low, "d_high": d_high,
+                "recipe": recipe, "t": t_part, "c": c_part,
+            }
 
-        def difference_planes(made):
-            e_planes, d_planes = made["e"], made["d"]
+        def low_difference(made):
             nc.gpsimd.tensor_tensor(
-                out=d_planes[:, 0, :], in0=e_planes[:, 0, :], in1=e_planes[:, 1, :], op=ALU.subtract
-            )
-            nc.gpsimd.tensor_tensor(
-                out=d_planes[:, 1:3, :], in0=e_planes[:, ORDER - 3 : ORDER - 1, :],
-                in1=e_planes[:, ORDER - 2 : ORDER, :], op=ALU.subtract,
+                out=made["d_low"][:], in0=made["e_low0"][:], in1=made["e_low1"][:], op=ALU.subtract
             )
 
-        def multiply(step, made):
+        def high_differences(made):
+            nc.gpsimd.tensor_tensor(
+                out=made["d_high"][:], in0=made["e_high"][:, 0:2, :], in1=made["e_high"][:, 1:3, :], op=ALU.subtract
+            )
+
+        def product(step, made, products, j):
             group, chunk = step
-            products = stage.tile([P, TERMS, CHUNK], F32, tag="products")
             cols = slice(chunk * CHUNK, (chunk + 1) * CHUNK)
-            for k in range(TERMS):
-                g_k = mx_psum.tile([P, CHUNK], F32, tag="g_k")
-                nc.tensor.matmul_mx(
-                    out=g_k[:],
-                    lhsT=wc_codes[:, group, k * P : (k + 1) * P].bitcast(E4M3_X4),
-                    lhsT_scale=wc_scales[:, group, k * P : (k + 1) * P],
-                    rhs=g_codes[:, cols].bitcast(E5M2_X4),
-                    rhs_scale=g_scales[:, cols],
-                    start=True,
-                    stop=True,
-                )
-                form, plane, number = made["recipe"][k]
-                if form == "times":
-                    nc.vector.scalar_tensor_tensor(
-                        out=products[:, k, :], in0=g_k[:], scalar=number, in1=plane, op0=ALU.mult, op1=ALU.mult
-                    )
-                else:
-                    nc.vector.scalar_tensor_tensor(
-                        out=products[:, k, :], in0=plane, scalar=number, in1=g_k[:], op0=ALU.subtract, op1=ALU.mult
-                    )
-            return products
+            g_k = mx_psum.tile([P, CHUNK], F32, tag="g_k")
+            nc.tensor.matmul_mx(
+                out=g_k[:],
+                lhsT=wc_codes[:, group, j * P : (j + 1) * P].bitcast(E4M3_X4),
+                lhsT_scale=wc_scales[:, group, j * P : (j + 1) * P],
+                rhs=g_codes[:, cols].bitcast(E5M2_X4),
+                rhs_scale=g_scales[:, cols],
+                start=True,
+                stop=True,
+            )
+            form, plane, number = made["recipe"][K_ORDER[j]]
+            nc.vector.scalar_tensor_tensor(
+                out=products[:, j, :], in0=plane, scalar=number, in1=g_k[:],
+                op0=ALU.mult if form == "times" else ALU.subtract, op1=ALU.mult,
+            )
 
-        def sum_and_store(step, made, products):
-            group, chunk = step
-            total = sum_psum.tile([P, BLOCKS, P], F32, tag="total")
-            for b in range(BLOCKS):
-                for k in range(TERMS):
+        def add_up(total, products, first, last):
+            for j in range(first, last):
+                for b in range(BLOCKS):
                     nc.tensor.matmul(
                         out=total[:, b, :],
-                        lhsT=products[:, k, b * P : (b + 1) * P],
+                        lhsT=products[:, j, b * P : (b + 1) * P],
                         rhs=ident_f32[:],
                         is_transpose=True,
-                        start=(k == 0),
-                        stop=(k == TERMS - 1),
+                        start=(j == 0 and b == 0),
+                        stop=(j == TERMS - 1 and b == BLOCKS - 1),
                     )
+
+        def scale_sum(made, total):
             scaled = stage.tile([P, BLOCKS, P], F32, tag="scaled")
             nc.vector.scalar_tensor_tensor(
                 out=scaled[:], in0=made["t"][:], scalar=1.0, in1=total[:], op0=ALU.subtract, op1=ALU.mult
             )
+            made["scaled"] = scaled
+
+        def finish(step, made):
+            group, chunk = step
             result = stage.tile([P, BLOCKS, P], F32, tag="result")
-            nc.gpsimd.tensor_tensor(out=result[:], in0=scaled[:], in1=made["c"][:], op=ALU.mult)
+            nc.gpsimd.tensor_tensor(out=result[:], in0=made["scaled"][:], in1=made["c"][:], op=ALU.mult)
             nc.sync.dma_start(
                 out=out[chunk * CHUNK : (chunk + 1) * CHUNK, group * P : (group + 1) * P].rearrange(
                     "(b p) i -> p b i", p=P
@@ -262,35 +278,86 @@ def tile_custombernsteinlayer_kernel(tc, x, weights, coeffs, grad_out, out):
                 in_=result[:],
             )
 
-        load_coeffs(0)
-        nc.sync.dma_start(out=w_rows[:], in_=weights.rearrange("(p t) i -> p t i", t=PACK))
-        load_tokens(0)
-        load_tokens(1)
-        load_coeffs(1)
-        load_tokens(2)
-        load_tokens(3)
-
         steps = [(group, chunk) for group in range(N_GROUPS) for chunk in range(N_CHUNKS)]
+        last = len(steps)
+        ctx.enter_context(tc.manual_schedule())
+
+        load_x(0)
+        load_grad(0)
+        nc.sync.dma_start(out=w_rows[:], in_=weights.rearrange("(p t) i -> p t i", t=PACK))
+        load_coeffs(0)
+        load_x(1)
+        load_grad(1)
+        load_x(2)
+        load_coeffs(1)
+        load_grad(2)
+        load_x(3)
+        load_grad(3)
+
         made = {}
-        products = {}
-
+        x_t = {}
         clamp_x(0)
-        made[0] = scalar_planes(steps[0])
+        x_t[0] = turn_x(steps[0])
+        made[0] = scalar_planes(steps[0], x_t[0])
+        turn_grad(0, 0)
+        turn_grad(0, 1)
         nc.vector.tensor_copy(out=w_words[:], in_=w_rows[:].rearrange("p t i -> p i t"))
-        quantise_wc(0)
         quantise_grad(0)
-        difference_planes(made[0])
-        for s in range(1, AHEAD):
-            first_use(steps[s])
+        clamp_x(1)
+        x_t[1] = turn_x(steps[1])
+        for part in range(len(PARTS)):
+            regroup(0, part)
+            if part == 1:
+                low_difference(made[0])
+            multiply_wc(0, part)
+            if part >= 1:
+                quantise_wc(0, part - 1)
+        high_differences(made[0])
 
-        for s in range(len(steps) + 1):
-            if s + 1 < len(steps):
-                made[s + 1] = scalar_planes(steps[s + 1])
-            if s < len(steps):
-                products[s] = multiply(steps[s], made[s])
-            if s + 1 < len(steps):
-                difference_planes(made[s + 1])
-            if s + AHEAD < len(steps):
-                first_use(steps[s + AHEAD])
+        products = {}
+        totals = {}
+        for s in range(last + 1):
+            live = s < last
+            if live:
+                group, chunk = steps[s]
+                parts = []
+                if group + 1 < N_GROUPS:
+                    parts = [chunk] if chunk + 1 < N_CHUNKS else [chunk, chunk + 1]
+                if s + 1 < last:
+                    made[s + 1] = scalar_planes(steps[s + 1], x_t[s + 1])
+                for part in parts:
+                    regroup(group + 1, part)
+                if s + 1 < last:
+                    low_difference(made[s + 1])
+                now = stage.tile([P, TERMS, CHUNK], F32, tag="products")
+                products[s] = now
+                for j in range(5):
+                    product(steps[s], made[s], now, j)
+                    if s == 0 and j == 2:
+                        quantise_wc(0, len(PARTS) - 1)
+                if s + 2 < last:
+                    if s + 2 < N_CHUNKS:
+                        clamp_x(s + 2)
+                    x_t[s + 2] = turn_x(steps[s + 2])
             if s >= 1:
-                sum_and_store(steps[s - 1], made[s - 1], products[s - 1])
+                add_up(totals[s - 1], products[s - 1], EARLY, TERMS)
+                scale_sum(made[s - 1], totals[s - 1])
+                finish(steps[s - 1], made[s - 1])
+            if live:
+                if s + 1 < last:
+                    high_differences(made[s + 1])
+                for part in parts:
+                    multiply_wc(group + 1, part)
+                for j in range(5, TERMS):
+                    product(steps[s], made[s], now, j)
+                for part in parts:
+                    quantise_wc(group + 1, part)
+                if chunk == N_CHUNKS - 1 and group + 2 < N_GROUPS:
+                    load_coeffs(group + 2)
+                total = sum_psum.tile([P, BLOCKS, P], F32, tag="total")
+                totals[s] = total
+                add_up(total, now, 0, EARLY)
+                if group == 0 and chunk + 1 < N_CHUNKS:
+                    turn_grad(chunk + 1, 0)
+                    turn_grad(chunk + 1, 1)
+                    quantise_grad(chunk + 1)

@@ -25,8 +25,8 @@ FLAT = 3
 X_LIMIT = 8.0
 NEGATED = (FLAT - 1, FLAT)
 K_ORDER = (0, ORDER, FLAT, FLAT + 1, 1, FLAT - 1, FLAT + 2, ORDER - 2, ORDER - 1)
-PARTS = ((0, 2), (2, 2), (4, 2), (6, 2), (8, 1))
-EARLY = 4
+HEAD_PARTS = ((0, 1), (1, 1), (2, 2), (4, 2), (6, 2), (8, 1))
+STEP_PARTS = (((0, 2),), ((2, 2),), ((4, 2),), ((6, 2), (8, 1)))
 
 FLOPS = 2 * TOKENS * OUTPUTS * FEATURES * TERMS
 
@@ -47,9 +47,9 @@ def tile_custombernsteinlayer_kernel(tc, x, weights, coeffs, grad_out, out):
     with ExitStack() as ctx:
         keep = ctx.enter_context(tc.tile_pool(name="keep", bufs=1))
         stage = ctx.enter_context(tc.tile_pool(name="stage", bufs=2))
-        mx_psum = ctx.enter_context(tc.psum_pool(name="mx_psum", bufs=5))
+        mx_psum = ctx.enter_context(tc.psum_pool(name="mx_psum", bufs=4))
         tr_psum = ctx.enter_context(tc.psum_pool(name="tr_psum", bufs=2))
-        sum_psum = ctx.enter_context(tc.psum_pool(name="sum_psum", bufs=1))
+        sum_psum = ctx.enter_context(tc.psum_pool(name="sum_psum", bufs=2))
 
         ident_f32 = keep.tile([P, P], F32)
         make_identity(nc, ident_f32[:])
@@ -59,6 +59,7 @@ def tile_custombernsteinlayer_kernel(tc, x, weights, coeffs, grad_out, out):
         x_rows = keep.tile([P, N_CHUNKS * BLOCKS, FEATURES], BF16)
         w_rows = keep.tile([P, PACK, FEATURES], BF16)
         w_words = keep.tile([P, FEATURES, PACK], BF16)
+        w_negated = keep.tile([P, FEATURES, PACK], BF16)
         g_codes = keep.tile([P, TOKENS], U32, align_bytes=64)
         g_scales = keep.tile([P, TOKENS], U8, align_bytes=64)
         wc_codes = keep.tile([P, N_GROUPS, TERMS * P], U32, align_bytes=64)
@@ -70,6 +71,7 @@ def tile_custombernsteinlayer_kernel(tc, x, weights, coeffs, grad_out, out):
         grad_tiles = {}
         gq_tiles = {}
         wq_tiles = {}
+        turned = {}
 
         def load_coeffs(group):
             co = stage.tile([P, PACK, group_cols], BF16, tag="co")
@@ -87,30 +89,29 @@ def tile_custombernsteinlayer_kernel(tc, x, weights, coeffs, grad_out, out):
             nc.sync.dma_start(out=g_rows[:], in_=grad_out[rows, :].rearrange("(b p) o -> p b o", p=P))
             grad_tiles[chunk] = g_rows
 
-        def regroup(group, part):
-            first, count = PARTS[part]
-            wq = stage.tile([P, 2, P, PACK], BF16, tag="wq", bufs=3, align_bytes=64)
+        def multiply_wc(group, part):
+            first, count = part
+            wq = stage.tile([P, 2, P, PACK], BF16, tag="wq", bufs=4, align_bytes=64)
             by_plane = coeff_tiles[group][:].rearrange("p t (i k) -> p k i t", k=TERMS)
             for j in range(count):
                 k = K_ORDER[first + j]
-                nc.gpsimd.tensor_scalar(
-                    out=wq[:, j, :, :], in0=by_plane[:, k, :, :],
-                    scalar1=-1.0 if k in NEGATED else 1.0, scalar2=0.0, op0=ALU.mult, op1=ALU.add,
+                words = w_negated if k in NEGATED else w_words
+                nc.gpsimd.tensor_tensor(
+                    out=wq[:, j, :, :], in0=by_plane[:, k, :, :], in1=words[:, group * P : (group + 1) * P, :], op=ALU.mult
                 )
             wq_tiles[group, part] = wq
 
-        def multiply_wc(group, part):
-            count = PARTS[part][1]
-            wq = wq_tiles[group, part]
+        def multiply_first(part):
+            first, count = part
+            wq = stage.tile([P, 2, P, PACK], BF16, tag="wq", bufs=4, align_bytes=64)
+            by_plane = coeff_tiles[0][:].rearrange("p t (i k) -> p k i t", k=TERMS)
             nc.vector.tensor_tensor(
-                out=wq[:, 0:count, :, :],
-                in0=wq[:, 0:count, :, :],
-                in1=w_words[:, group * P : (group + 1) * P, :].unsqueeze(1).to_broadcast([P, count, P, PACK]),
-                op=ALU.mult,
+                out=wq[:, 0, :, :], in0=by_plane[:, K_ORDER[first], :, :], in1=w_words[:, 0:P, :], op=ALU.mult
             )
+            wq_tiles[0, part] = wq
 
         def quantise_wc(group, part):
-            first, count = PARTS[part]
+            first, count = part
             cols = slice(first * P, (first + count) * P)
             flat = wq_tiles[group, part][:].rearrange("p k i t -> p (k i t)")
             nc.vector.quantize_mx(
@@ -127,11 +128,7 @@ def tile_custombernsteinlayer_kernel(tc, x, weights, coeffs, grad_out, out):
             )
 
         def turn_grad(chunk, half):
-            if half == 0:
-                gq = stage.tile([P, CHUNK * PACK], BF16, tag="gq", align_bytes=64)
-                gq_tiles[chunk] = gq
             g_words = grad_tiles[chunk][:].bitcast(F32)
-            gq_words = gq_tiles[chunk][:].bitcast(F32).rearrange("p (n u) -> p n u", u=2)
             g_t = mx_psum.tile([P, 2, 2 * P], F32, tag="g_k")
             for b in range(2):
                 for u in range(2):
@@ -140,8 +137,16 @@ def tile_custombernsteinlayer_kernel(tc, x, weights, coeffs, grad_out, out):
                         in_=g_words[:, 2 * half + b, u : 2 * P : 2],
                         identity=ident_f32[:],
                     )
+            turned[chunk, half] = g_t
+
+        def gather_grad(chunk, half):
+            if half == 0:
+                gq = stage.tile([P, CHUNK * PACK], BF16, tag="gq", align_bytes=64)
+                gq_tiles[chunk] = gq
+            gq_words = gq_tiles[chunk][:].bitcast(F32).rearrange("p (n u) -> p n u", u=2)
             nc.vector.tensor_copy(
-                out=gq_words[:, half * 2 * P : (half + 1) * 2 * P, :], in_=g_t[:].rearrange("p u n -> p n u")
+                out=gq_words[:, half * 2 * P : (half + 1) * 2 * P, :],
+                in_=turned[chunk, half][:].rearrange("p u n -> p n u"),
             )
 
         def quantise_grad(chunk):
@@ -225,11 +230,13 @@ def tile_custombernsteinlayer_kernel(tc, x, weights, coeffs, grad_out, out):
             )
 
         def high_differences(made):
-            nc.gpsimd.tensor_tensor(
-                out=made["d_high"][:], in0=made["e_high"][:, 0:2, :], in1=made["e_high"][:, 1:3, :], op=ALU.subtract
-            )
+            for j in range(2):
+                nc.gpsimd.tensor_tensor(
+                    out=made["d_high"][:, j, :], in0=made["e_high"][:, j, :], in1=made["e_high"][:, j + 1, :],
+                    op=ALU.subtract,
+                )
 
-        def product(step, made, products, j):
+        def multiply(step, j):
             group, chunk = step
             cols = slice(chunk * CHUNK, (chunk + 1) * CHUNK)
             g_k = mx_psum.tile([P, CHUNK], F32, tag="g_k")
@@ -242,6 +249,9 @@ def tile_custombernsteinlayer_kernel(tc, x, weights, coeffs, grad_out, out):
                 start=True,
                 stop=True,
             )
+            return g_k
+
+        def weigh(g_k, made, products, j):
             form, plane, number = made["recipe"][K_ORDER[j]]
             nc.vector.scalar_tensor_tensor(
                 out=products[:, j, :], in0=plane, scalar=number, in1=g_k[:],
@@ -299,65 +309,81 @@ def tile_custombernsteinlayer_kernel(tc, x, weights, coeffs, grad_out, out):
         clamp_x(0)
         x_t[0] = turn_x(steps[0])
         made[0] = scalar_planes(steps[0], x_t[0])
-        turn_grad(0, 0)
-        turn_grad(0, 1)
+        for half in range(2):
+            turn_grad(0, half)
+        for half in range(2):
+            gather_grad(0, half)
         nc.vector.tensor_copy(out=w_words[:], in_=w_rows[:].rearrange("p t i -> p i t"))
+        nc.vector.tensor_scalar(
+            out=w_negated[:], in0=w_words[:], scalar1=-1.0, scalar2=0.0, op0=ALU.mult, op1=ALU.add
+        )
         quantise_grad(0)
+        multiply_first(HEAD_PARTS[0])
+        multiply_first(HEAD_PARTS[1])
         clamp_x(1)
         x_t[1] = turn_x(steps[1])
-        for part in range(len(PARTS)):
-            regroup(0, part)
-            if part == 1:
-                low_difference(made[0])
-            multiply_wc(0, part)
-            if part >= 1:
-                quantise_wc(0, part - 1)
+        multiply_wc(0, HEAD_PARTS[2])
+        low_difference(made[0])
+        multiply_wc(0, HEAD_PARTS[3])
+        multiply_wc(0, HEAD_PARTS[4])
         high_differences(made[0])
-
+        multiply_wc(0, HEAD_PARTS[5])
+        quantise_wc(0, HEAD_PARTS[0])
+        head_work = {max(0, part[0] - 1): part for part in HEAD_PARTS[1:]}
+        slots = [(s, j) for s in range(last) for j in range(TERMS)]
+        banks = {}
+        ready = 1
         products = {}
         totals = {}
-        for s in range(last + 1):
-            live = s < last
-            if live:
-                group, chunk = steps[s]
-                parts = []
-                if group + 1 < N_GROUPS:
-                    parts = [chunk] if chunk + 1 < N_CHUNKS else [chunk, chunk + 1]
+        for n, (s, j) in enumerate(slots):
+            group, chunk = steps[s]
+            parts = STEP_PARTS[chunk] if group + 1 < N_GROUPS else ()
+            turning = group == 0 and chunk + 1 < N_CHUNKS
+            if j == 0:
+                if chunk == 0 and group + 2 < N_GROUPS:
+                    load_coeffs(group + 2)
                 if s + 1 < last:
                     made[s + 1] = scalar_planes(steps[s + 1], x_t[s + 1])
                 for part in parts:
-                    regroup(group + 1, part)
+                    multiply_wc(group + 1, part)
                 if s + 1 < last:
                     low_difference(made[s + 1])
-                now = stage.tile([P, TERMS, CHUNK], F32, tag="products")
-                products[s] = now
-                for j in range(5):
-                    product(steps[s], made[s], now, j)
-                    if s == 0 and j == 2:
-                        quantise_wc(0, len(PARTS) - 1)
-                if s + 2 < last:
-                    if s + 2 < N_CHUNKS:
-                        clamp_x(s + 2)
-                    x_t[s + 2] = turn_x(steps[s + 2])
-            if s >= 1:
-                add_up(totals[s - 1], products[s - 1], EARLY, TERMS)
+                    high_differences(made[s + 1])
+                product_tile = stage.tile([P, TERMS, CHUNK], F32, tag="products")
+                products[s] = product_tile
+            if s == 0 and j in head_work:
+                quantise_wc(0, head_work[j])
+                ready = sum(head_work[j])
+            if n not in banks:
+                banks[n] = multiply(steps[s], j)
+            weigh(banks[n], made[s], products[s], j)
+            if turning and j in (3, 6):
+                gather_grad(chunk + 1, j // 3 - 1)
+            if turning and j == 7:
+                quantise_grad(chunk + 1)
+            if not turning or j >= 7:
+                ready = TERMS * (s + 2)
+            for ahead in range(n + 1, min(n + 5, len(slots), ready)):
+                if ahead not in banks:
+                    ahead_s, ahead_j = slots[ahead]
+                    banks[ahead] = multiply(steps[ahead_s], ahead_j)
+            if turning and j in (1, 4):
+                turn_grad(chunk + 1, j // 4)
+            if j == 1 and s >= 1:
                 scale_sum(made[s - 1], totals[s - 1])
                 finish(steps[s - 1], made[s - 1])
-            if live:
-                if s + 1 < last:
-                    high_differences(made[s + 1])
-                for part in parts:
-                    multiply_wc(group + 1, part)
-                for j in range(5, TERMS):
-                    product(steps[s], made[s], now, j)
-                for part in parts:
-                    quantise_wc(group + 1, part)
-                if chunk == N_CHUNKS - 1 and group + 2 < N_GROUPS:
-                    load_coeffs(group + 2)
+            if j == 3 and s + 2 < last:
+                if s + 2 < N_CHUNKS:
+                    clamp_x(s + 2)
+                x_t[s + 2] = turn_x(steps[s + 2])
+            if j == 1:
                 total = sum_psum.tile([P, BLOCKS, P], F32, tag="total")
                 totals[s] = total
-                add_up(total, now, 0, EARLY)
-                if group == 0 and chunk + 1 < N_CHUNKS:
-                    turn_grad(chunk + 1, 0)
-                    turn_grad(chunk + 1, 1)
-                    quantise_grad(chunk + 1)
+            if j % 2 == 1:
+                add_up(totals[s], products[s], j - 1, j + 1)
+            if j == TERMS - 1:
+                add_up(totals[s], products[s], j, j + 1)
+                for part in parts:
+                    quantise_wc(group + 1, part)
+        scale_sum(made[last - 1], totals[last - 1])
+        finish(steps[last - 1], made[last - 1])

@@ -22,6 +22,7 @@ BLOCKS = CHUNK // P
 N_CHUNKS = TOKENS // CHUNK
 N_GROUPS = FEATURES // P
 FLAT = 3
+RUN = 3
 X_LIMIT = 8.0
 NEGATED = (FLAT - 1, FLAT)
 K_ORDER = (0, ORDER, FLAT, FLAT + 1, 1, FLAT - 1, FLAT + 2, ORDER - 2, ORDER - 1)
@@ -47,9 +48,9 @@ def tile_custombernsteinlayer_kernel(tc, x, weights, coeffs, grad_out, out):
     with ExitStack() as ctx:
         keep = ctx.enter_context(tc.tile_pool(name="keep", bufs=1))
         stage = ctx.enter_context(tc.tile_pool(name="stage", bufs=2))
-        mx_psum = ctx.enter_context(tc.psum_pool(name="mx_psum", bufs=4))
+        mx_psum = ctx.enter_context(tc.psum_pool(name="mx_psum", bufs=5))
         tr_psum = ctx.enter_context(tc.psum_pool(name="tr_psum", bufs=2))
-        sum_psum = ctx.enter_context(tc.psum_pool(name="sum_psum", bufs=2))
+        sum_psum = ctx.enter_context(tc.psum_pool(name="sum_psum", bufs=1))
 
         ident_f32 = keep.tile([P, P], F32)
         make_identity(nc, ident_f32[:])
@@ -59,7 +60,6 @@ def tile_custombernsteinlayer_kernel(tc, x, weights, coeffs, grad_out, out):
         x_rows = keep.tile([P, N_CHUNKS * BLOCKS, FEATURES], BF16)
         w_rows = keep.tile([P, PACK, FEATURES], BF16)
         w_words = keep.tile([P, FEATURES, PACK], BF16)
-        w_negated = keep.tile([P, FEATURES, PACK], BF16)
         g_codes = keep.tile([P, TOKENS], U32, align_bytes=64)
         g_scales = keep.tile([P, TOKENS], U8, align_bytes=64)
         wc_codes = keep.tile([P, N_GROUPS, TERMS * P], U32, align_bytes=64)
@@ -89,17 +89,27 @@ def tile_custombernsteinlayer_kernel(tc, x, weights, coeffs, grad_out, out):
             nc.sync.dma_start(out=g_rows[:], in_=grad_out[rows, :].rearrange("(b p) o -> p b o", p=P))
             grad_tiles[chunk] = g_rows
 
-        def multiply_wc(group, part):
+        def regroup(group, part):
             first, count = part
             wq = stage.tile([P, 2, P, PACK], BF16, tag="wq", bufs=4, align_bytes=64)
             by_plane = coeff_tiles[group][:].rearrange("p t (i k) -> p k i t", k=TERMS)
             for j in range(count):
                 k = K_ORDER[first + j]
-                words = w_negated if k in NEGATED else w_words
-                nc.gpsimd.tensor_tensor(
-                    out=wq[:, j, :, :], in0=by_plane[:, k, :, :], in1=words[:, group * P : (group + 1) * P, :], op=ALU.mult
+                nc.gpsimd.tensor_scalar(
+                    out=wq[:, j, :, :], in0=by_plane[:, k, :, :],
+                    scalar1=-1.0 if k in NEGATED else 1.0, scalar2=0.0, op0=ALU.mult, op1=ALU.add,
                 )
             wq_tiles[group, part] = wq
+
+        def multiply_wc(group, part):
+            count = part[1]
+            wq = wq_tiles[group, part]
+            nc.vector.tensor_tensor(
+                out=wq[:, 0:count, :, :],
+                in0=wq[:, 0:count, :, :],
+                in1=w_words[:, group * P : (group + 1) * P, :].unsqueeze(1).to_broadcast([P, count, P, PACK]),
+                op=ALU.mult,
+            )
 
         def multiply_first(part):
             first, count = part
@@ -236,10 +246,12 @@ def tile_custombernsteinlayer_kernel(tc, x, weights, coeffs, grad_out, out):
                     op=ALU.subtract,
                 )
 
-        def multiply(step, j):
+        def multiply(step, j, busy):
             group, chunk = step
             cols = slice(chunk * CHUNK, (chunk + 1) * CHUNK)
             g_k = mx_psum.tile([P, CHUNK], F32, tag="g_k")
+            if busy:
+                nc.tensor.matmul(out=g_k[:, 0:P], lhsT=ident_f32[:], rhs=ident_f32[:], start=True, stop=True)
             nc.tensor.matmul_mx(
                 out=g_k[:],
                 lhsT=wc_codes[:, group, j * P : (j + 1) * P].bitcast(E4M3_X4),
@@ -314,25 +326,27 @@ def tile_custombernsteinlayer_kernel(tc, x, weights, coeffs, grad_out, out):
         for half in range(2):
             gather_grad(0, half)
         nc.vector.tensor_copy(out=w_words[:], in_=w_rows[:].rearrange("p t i -> p i t"))
-        nc.vector.tensor_scalar(
-            out=w_negated[:], in0=w_words[:], scalar1=-1.0, scalar2=0.0, op0=ALU.mult, op1=ALU.add
-        )
         quantise_grad(0)
+        for i in range(8):
+            warm = mx_psum.tile([P, CHUNK], F32, tag="g_k")
+            nc.tensor.matmul(out=warm[:], lhsT=ident_bf16[:], rhs=w_rows[:, 0, :], start=True, stop=True)
         multiply_first(HEAD_PARTS[0])
         multiply_first(HEAD_PARTS[1])
         clamp_x(1)
         x_t[1] = turn_x(steps[1])
-        multiply_wc(0, HEAD_PARTS[2])
+        regroup(0, HEAD_PARTS[2])
         low_difference(made[0])
-        multiply_wc(0, HEAD_PARTS[3])
-        multiply_wc(0, HEAD_PARTS[4])
+        regroup(0, HEAD_PARTS[3])
         high_differences(made[0])
-        multiply_wc(0, HEAD_PARTS[5])
+        regroup(0, HEAD_PARTS[4])
+        regroup(0, HEAD_PARTS[5])
         quantise_wc(0, HEAD_PARTS[0])
-        head_work = {max(0, part[0] - 1): part for part in HEAD_PARTS[1:]}
+        quantise_wc(0, HEAD_PARTS[1])
+        head_multiply = {part[0] - 2: part for part in HEAD_PARTS[2:]}
+        head_quantise = {part[0] - 1: part for part in HEAD_PARTS[2:]}
         slots = [(s, j) for s in range(last) for j in range(TERMS)]
         banks = {}
-        ready = 1
+        ready = 2
         products = {}
         totals = {}
         for n, (s, j) in enumerate(slots):
@@ -345,44 +359,51 @@ def tile_custombernsteinlayer_kernel(tc, x, weights, coeffs, grad_out, out):
                 if s + 1 < last:
                     made[s + 1] = scalar_planes(steps[s + 1], x_t[s + 1])
                 for part in parts:
-                    multiply_wc(group + 1, part)
+                    regroup(group + 1, part)
                 if s + 1 < last:
                     low_difference(made[s + 1])
                     high_differences(made[s + 1])
                 product_tile = stage.tile([P, TERMS, CHUNK], F32, tag="products")
                 products[s] = product_tile
-            if s == 0 and j in head_work:
-                quantise_wc(0, head_work[j])
-                ready = sum(head_work[j])
+            if s == 0 and j in head_quantise:
+                quantise_wc(0, head_quantise[j])
+                ready = sum(head_quantise[j])
+            if s == 0 and j in head_multiply:
+                multiply_wc(0, head_multiply[j])
             if n not in banks:
-                banks[n] = multiply(steps[s], j)
+                banks[n] = multiply(steps[s], j, False)
             weigh(banks[n], made[s], products[s], j)
-            if turning and j in (3, 6):
-                gather_grad(chunk + 1, j // 3 - 1)
-            if turning and j == 7:
-                quantise_grad(chunk + 1)
-            if not turning or j >= 7:
-                ready = TERMS * (s + 2)
-            for ahead in range(n + 1, min(n + 5, len(slots), ready)):
-                if ahead not in banks:
-                    ahead_s, ahead_j = slots[ahead]
-                    banks[ahead] = multiply(steps[ahead_s], ahead_j)
-            if turning and j in (1, 4):
-                turn_grad(chunk + 1, j // 4)
-            if j == 1 and s >= 1:
+            if j == 2 and s >= 1:
                 scale_sum(made[s - 1], totals[s - 1])
                 finish(steps[s - 1], made[s - 1])
-            if j == 3 and s + 2 < last:
+            if turning and j in (2, 3):
+                gather_grad(chunk + 1, j - 2)
+            if turning and j == 4:
+                quantise_grad(chunk + 1)
+            if j == 6:
+                for part in parts:
+                    multiply_wc(group + 1, part)
+            if (not turning and j >= 4) or j == 8 or (turning and j >= 5 and s > 0):
+                ready = TERMS * (s + 2)
+            if j % RUN == RUN - 1 or s == 0:
+                first_of_run = True
+                for ahead in range(n + 1, min(n + 6, len(slots), ready)):
+                    if ahead not in banks:
+                        ahead_s, ahead_j = slots[ahead]
+                        banks[ahead] = multiply(steps[ahead_s], ahead_j, first_of_run)
+                        first_of_run = False
+            if turning and j in (0, 1):
+                turn_grad(chunk + 1, j)
+            if j == 5 and s + 2 < last:
                 if s + 2 < N_CHUNKS:
                     clamp_x(s + 2)
                 x_t[s + 2] = turn_x(steps[s + 2])
-            if j == 1:
-                total = sum_psum.tile([P, BLOCKS, P], F32, tag="total")
-                totals[s] = total
-            if j % 2 == 1:
-                add_up(totals[s], products[s], j - 1, j + 1)
+            if j % RUN == RUN - 1:
+                if j == RUN - 1:
+                    total = sum_psum.tile([P, BLOCKS, P], F32, tag="total")
+                    totals[s] = total
+                add_up(totals[s], products[s], j + 1 - RUN, j + 1)
             if j == TERMS - 1:
-                add_up(totals[s], products[s], j, j + 1)
                 for part in parts:
                     quantise_wc(group + 1, part)
         scale_sum(made[last - 1], totals[last - 1])

@@ -24,8 +24,12 @@ N_GROUPS = FEATURES // P
 FLAT = 3
 RUN = 3
 X_LIMIT = 8.0
-NEGATED = (FLAT - 1, FLAT)
-K_ORDER = (0, ORDER, FLAT, FLAT + 1, 1, FLAT - 1, FLAT + 2, ORDER - 2, ORDER - 1)
+OPERANDS = ((0, 8.0), (1, -1.0), (3, -1.0), (8, -8.0), (7, 1.0), (4, 1.0), (2, -1.0), (5, 1.0), (6, 1.0))
+PRODUCTS = (
+    ("e0", (0, 1)), ("e1", (1,)), ("line_low", (2,)),
+    ("e7", (3, 4)), ("e6", (4,)), ("line_high", (5,)),
+    ("square_low", (6,)), ("square_high", (7,)), ("d6", (8,)),
+)
 HEAD_PARTS = ((0, 1), (1, 1), (2, 2), (4, 2), (6, 2), (8, 1))
 STEP_PARTS = (((0, 2),), ((2, 2),), ((4, 2),), ((6, 2), (8, 1)))
 
@@ -94,10 +98,10 @@ def tile_custombernsteinlayer_kernel(tc, x, weights, coeffs, grad_out, out):
             wq = stage.tile([P, 2, P, PACK], BF16, tag="wq", bufs=4, align_bytes=64)
             by_plane = coeff_tiles[group][:].rearrange("p t (i k) -> p k i t", k=TERMS)
             for j in range(count):
-                k = K_ORDER[first + j]
+                k, factor = OPERANDS[first + j]
                 nc.gpsimd.tensor_scalar(
                     out=wq[:, j, :, :], in0=by_plane[:, k, :, :],
-                    scalar1=-1.0 if k in NEGATED else 1.0, scalar2=0.0, op0=ALU.mult, op1=ALU.add,
+                    scalar1=factor, scalar2=0.0, op0=ALU.mult, op1=ALU.add,
                 )
             wq_tiles[group, part] = wq
 
@@ -115,8 +119,10 @@ def tile_custombernsteinlayer_kernel(tc, x, weights, coeffs, grad_out, out):
             first, count = part
             wq = stage.tile([P, 2, P, PACK], BF16, tag="wq", bufs=4, align_bytes=64)
             by_plane = coeff_tiles[0][:].rearrange("p t (i k) -> p k i t", k=TERMS)
-            nc.vector.tensor_tensor(
-                out=wq[:, 0, :, :], in0=by_plane[:, K_ORDER[first], :, :], in1=w_words[:, 0:P, :], op=ALU.mult
+            k, factor = OPERANDS[first]
+            nc.vector.scalar_tensor_tensor(
+                out=wq[:, 0, :, :], in0=by_plane[:, k, :, :], scalar=factor, in1=w_words[:, 0:P, :],
+                op0=ALU.mult, op1=ALU.mult,
             )
             wq_tiles[0, part] = wq
 
@@ -185,8 +191,7 @@ def tile_custombernsteinlayer_kernel(tc, x, weights, coeffs, grad_out, out):
             line_high = stage.tile([P, CHUNK], F32, tag="line_high")
             square_low = stage.tile([P, CHUNK], F32, tag="square_low")
             square_high = stage.tile([P, CHUNK], F32, tag="square_high")
-            d_low = stage.tile([P, CHUNK], F32, tag="d_low")
-            d_high = stage.tile([P, 2, CHUNK], F32, tag="d_high")
+            d_six = stage.tile([P, CHUNK], F32, tag="d_six")
             t_part = stage.tile([P, BLOCKS, P], F32, tag="t_part", bufs=3)
             c_part = stage.tile([P, BLOCKS, P], F32, tag="c_part", bufs=3)
             x_part = x_rows[:, chunk * BLOCKS : (chunk + 1) * BLOCKS, group * P : (group + 1) * P]
@@ -197,11 +202,11 @@ def tile_custombernsteinlayer_kernel(tc, x, weights, coeffs, grad_out, out):
                 )
 
             recipe = {
-                0: ("times", e_low0[:], gamma(0)),
-                1: ("times", d_low[:], -gamma(1)),
-                ORDER - 2: ("times", d_high[:, 0, :], -gamma(ORDER - 2)),
-                ORDER - 1: ("times", d_high[:, 1, :], -gamma(ORDER - 1)),
-                ORDER: ("times", e_high[:, 2, :], -gamma(ORDER)),
+                "e0": ("times", e_low0[:], 1.0),
+                "e1": ("times", e_low1[:], -1.0),
+                "d6": ("times", d_six[:], -gamma(ORDER - 2)),
+                "e6": ("times", e_high[:, 1, :], -1.0),
+                "e7": ("times", e_high[:, 2, :], 1.0),
             }
             exp_plane(e_low0[:], 0, binomial(ORDER - 1, 0))
             exp_plane(e_low1[:], 1, binomial(ORDER - 1, 1))
@@ -216,8 +221,8 @@ def tile_custombernsteinlayer_kernel(tc, x, weights, coeffs, grad_out, out):
                 k_far = k_near + side
                 middle = near / (2.0 * far)
                 root = math.sqrt(gamma(k_far) * far)
-                recipe[k_near] = ("minus", line[:], gamma(k_near) * flat)
-                recipe[k_far] = ("minus", square[:], gamma(k_far) * near * near / (4.0 * far))
+                recipe["line_low" if side < 0 else "line_high"] = ("minus", line[:], gamma(k_near) * flat)
+                recipe["square_low" if side < 0 else "square_high"] = ("minus", square[:], gamma(k_far) * near * near / (4.0 * far))
                 squares.append((square, line, root / (gamma(k_near) * near), -root * middle))
             nc.scalar.activation(out=t_part[:], in_=x_part, func=ACT.Tanh)
             exp_plane(line_low[:], FLAT - 1, gamma(FLAT) * binomial(ORDER - 1, FLAT - 1))
@@ -230,41 +235,34 @@ def tile_custombernsteinlayer_kernel(tc, x, weights, coeffs, grad_out, out):
             for square, line, scale, bias in squares[1:]:
                 nc.scalar.activation(out=square[:], in_=line[:], func=ACT.Square, scale=scale, bias=bias)
             return {
-                "e_low0": e_low0, "e_low1": e_low1, "e_high": e_high, "d_low": d_low, "d_high": d_high,
+                "e_high": e_high, "d_six": d_six,
                 "recipe": recipe, "t": t_part, "c": c_part,
             }
 
-        def low_difference(made):
+        def difference(made):
             nc.gpsimd.tensor_tensor(
-                out=made["d_low"][:], in0=made["e_low0"][:], in1=made["e_low1"][:], op=ALU.subtract
+                out=made["d_six"][:], in0=made["e_high"][:, 0, :], in1=made["e_high"][:, 1, :], op=ALU.subtract
             )
 
-        def high_differences(made):
-            for j in range(2):
-                nc.gpsimd.tensor_tensor(
-                    out=made["d_high"][:, j, :], in0=made["e_high"][:, j, :], in1=made["e_high"][:, j + 1, :],
-                    op=ALU.subtract,
-                )
-
-        def multiply(step, j, busy):
+        def multiply(step, j):
             group, chunk = step
             cols = slice(chunk * CHUNK, (chunk + 1) * CHUNK)
             g_k = mx_psum.tile([P, CHUNK], F32, tag="g_k")
-            if busy:
-                nc.tensor.matmul(out=g_k[:, 0:P], lhsT=ident_f32[:], rhs=ident_f32[:], start=True, stop=True)
-            nc.tensor.matmul_mx(
-                out=g_k[:],
-                lhsT=wc_codes[:, group, j * P : (j + 1) * P].bitcast(E4M3_X4),
-                lhsT_scale=wc_scales[:, group, j * P : (j + 1) * P],
-                rhs=g_codes[:, cols].bitcast(E5M2_X4),
-                rhs_scale=g_scales[:, cols],
-                start=True,
-                stop=True,
-            )
+            places = PRODUCTS[j][1]
+            for i, place in enumerate(places):
+                nc.tensor.matmul_mx(
+                    out=g_k[:],
+                    lhsT=wc_codes[:, group, place * P : (place + 1) * P].bitcast(E4M3_X4),
+                    lhsT_scale=wc_scales[:, group, place * P : (place + 1) * P],
+                    rhs=g_codes[:, cols].bitcast(E5M2_X4),
+                    rhs_scale=g_scales[:, cols],
+                    start=(i == 0),
+                    stop=(i == len(places) - 1),
+                )
             return g_k
 
         def weigh(g_k, made, products, j):
-            form, plane, number = made["recipe"][K_ORDER[j]]
+            form, plane, number = made["recipe"][PRODUCTS[j][0]]
             nc.vector.scalar_tensor_tensor(
                 out=products[:, j, :], in0=plane, scalar=number, in1=g_k[:],
                 op0=ALU.mult if form == "times" else ALU.subtract, op1=ALU.mult,
@@ -327,17 +325,13 @@ def tile_custombernsteinlayer_kernel(tc, x, weights, coeffs, grad_out, out):
             gather_grad(0, half)
         nc.vector.tensor_copy(out=w_words[:], in_=w_rows[:].rearrange("p t i -> p i t"))
         quantise_grad(0)
-        for i in range(8):
-            warm = mx_psum.tile([P, CHUNK], F32, tag="g_k")
-            nc.tensor.matmul(out=warm[:], lhsT=ident_bf16[:], rhs=w_rows[:, 0, :], start=True, stop=True)
         multiply_first(HEAD_PARTS[0])
         multiply_first(HEAD_PARTS[1])
         clamp_x(1)
         x_t[1] = turn_x(steps[1])
         regroup(0, HEAD_PARTS[2])
-        low_difference(made[0])
         regroup(0, HEAD_PARTS[3])
-        high_differences(made[0])
+        difference(made[0])
         regroup(0, HEAD_PARTS[4])
         regroup(0, HEAD_PARTS[5])
         quantise_wc(0, HEAD_PARTS[0])
@@ -361,17 +355,17 @@ def tile_custombernsteinlayer_kernel(tc, x, weights, coeffs, grad_out, out):
                 for part in parts:
                     regroup(group + 1, part)
                 if s + 1 < last:
-                    low_difference(made[s + 1])
-                    high_differences(made[s + 1])
+                    difference(made[s + 1])
                 product_tile = stage.tile([P, TERMS, CHUNK], F32, tag="products")
                 products[s] = product_tile
             if s == 0 and j in head_quantise:
                 quantise_wc(0, head_quantise[j])
-                ready = sum(head_quantise[j])
+                quantised = sum(head_quantise[j])
+                ready = sum(1 for product in PRODUCTS if max(product[1]) < quantised)
             if s == 0 and j in head_multiply:
                 multiply_wc(0, head_multiply[j])
             if n not in banks:
-                banks[n] = multiply(steps[s], j, False)
+                banks[n] = multiply(steps[s], j)
             weigh(banks[n], made[s], products[s], j)
             if j == 2 and s >= 1:
                 scale_sum(made[s - 1], totals[s - 1])
@@ -386,12 +380,10 @@ def tile_custombernsteinlayer_kernel(tc, x, weights, coeffs, grad_out, out):
             if (not turning and j >= 4) or j == 8 or (turning and j >= 5 and s > 0):
                 ready = TERMS * (s + 2)
             if j % RUN == RUN - 1 or s == 0:
-                first_of_run = True
                 for ahead in range(n + 1, min(n + 6, len(slots), ready)):
                     if ahead not in banks:
                         ahead_s, ahead_j = slots[ahead]
-                        banks[ahead] = multiply(steps[ahead_s], ahead_j, first_of_run)
-                        first_of_run = False
+                        banks[ahead] = multiply(steps[ahead_s], ahead_j)
             if turning and j in (0, 1):
                 turn_grad(chunk + 1, j)
             if j == 5 and s + 2 < last:

@@ -24,13 +24,22 @@ N_GROUPS = FEATURES // P
 FLAT = 3
 RUN = 3
 X_LIMIT = 8.0
-OPERANDS = ((0, 8.0), (1, -1.0), (3, -1.0), (8, -8.0), (7, 1.0), (4, 1.0), (2, -1.0), (5, 1.0), (6, 1.0))
+OPERANDS = ((0, 8.0), (1, -1.0), (2, -1.0), (3, -1.0), (4, 1.0), (5, 1.0), (6, 1.0), (7, 1.0), (8, -8.0))
 PRODUCTS = (
-    ("e0", (0, 1)), ("e1", (1,)), ("line_low", (2,)),
-    ("e7", (3, 4)), ("e6", (4,)), ("line_high", (5,)),
-    ("square_low", (6,)), ("square_high", (7,)), ("d6", (8,)),
+    ("e0", (0, 1)), ("e1", (1,)), ("line_low", (3,)),
+    ("square_low", (2,)), ("line_high", (4,)), ("square_high", (5,)),
+    ("e6", (7,)), ("e7", (7, 8)), ("d6", (6,)),
 )
-HEAD_PARTS = ((0, 1), (1, 1), (2, 2), (4, 2), (6, 2), (8, 1))
+LOW, HIGH = (1, 3), (4, 4)
+PIECES = 2
+
+
+def pieces(first, count):
+    width = P // PIECES
+    return tuple((first, count, i * width, width) for i in range(PIECES))
+
+
+STEP_REGROUPS = (((0, 1, 0, P),) + pieces(*LOW), pieces(*HIGH), ((8, 1, 0, P),), ())
 STEP_PARTS = (((0, 2),), ((2, 2),), ((4, 2),), ((6, 2), (8, 1)))
 
 FLOPS = 2 * TOKENS * OUTPUTS * FEATURES * TERMS
@@ -52,8 +61,8 @@ def tile_custombernsteinlayer_kernel(tc, x, weights, coeffs, grad_out, out):
     with ExitStack() as ctx:
         keep = ctx.enter_context(tc.tile_pool(name="keep", bufs=1))
         stage = ctx.enter_context(tc.tile_pool(name="stage", bufs=2))
-        mx_psum = ctx.enter_context(tc.psum_pool(name="mx_psum", bufs=5))
-        tr_psum = ctx.enter_context(tc.psum_pool(name="tr_psum", bufs=2))
+        mx_psum = ctx.enter_context(tc.psum_pool(name="mx_psum", bufs=6))
+        tr_psum = ctx.enter_context(tc.psum_pool(name="tr_psum", bufs=1))
         sum_psum = ctx.enter_context(tc.psum_pool(name="sum_psum", bufs=1))
 
         ident_f32 = keep.tile([P, P], F32)
@@ -62,7 +71,8 @@ def tile_custombernsteinlayer_kernel(tc, x, weights, coeffs, grad_out, out):
         make_identity(nc, ident_bf16[:])
 
         x_rows = keep.tile([P, N_CHUNKS * BLOCKS, FEATURES], BF16)
-        w_rows = keep.tile([P, PACK, FEATURES], BF16)
+        w_first = keep.tile([P, PACK, P], BF16)
+        w_later = keep.tile([P, PACK, FEATURES - P], BF16)
         w_words = keep.tile([P, FEATURES, PACK], BF16)
         g_codes = keep.tile([P, TOKENS], U32, align_bytes=64)
         g_scales = keep.tile([P, TOKENS], U8, align_bytes=64)
@@ -82,6 +92,9 @@ def tile_custombernsteinlayer_kernel(tc, x, weights, coeffs, grad_out, out):
             nc.sync.dma_start(out=co[:], in_=coeff_view[:, :, group * group_cols : (group + 1) * group_cols])
             coeff_tiles[group] = co
 
+        def load_weights(w_rows, first, end):
+            nc.sync.dma_start(out=w_rows[:], in_=weights.rearrange("(p t) i -> p t i", t=PACK)[:, :, first:end])
+
         def load_x(chunk):
             rows = slice(chunk * CHUNK, (chunk + 1) * CHUNK)
             blocks = slice(chunk * BLOCKS, (chunk + 1) * BLOCKS)
@@ -93,54 +106,49 @@ def tile_custombernsteinlayer_kernel(tc, x, weights, coeffs, grad_out, out):
             nc.sync.dma_start(out=g_rows[:], in_=grad_out[rows, :].rearrange("(b p) o -> p b o", p=P))
             grad_tiles[chunk] = g_rows
 
-        def regroup(group, part):
-            first, count = part
-            wq = stage.tile([P, 2, P, PACK], BF16, tag="wq", bufs=4, align_bytes=64)
-            by_plane = coeff_tiles[group][:].rearrange("p t (i k) -> p k i t", k=TERMS)
-            for j in range(count):
-                k, factor = OPERANDS[first + j]
-                nc.gpsimd.tensor_scalar(
-                    out=wq[:, j, :, :], in0=by_plane[:, k, :, :],
-                    scalar1=factor, scalar2=0.0, op0=ALU.mult, op1=ALU.add,
-                )
-            wq_tiles[group, part] = wq
+        def regroup(group, block):
+            first, count, feature, features = block
+            rows = slice(feature, feature + features)
+            by_feature = coeff_tiles[group][:].rearrange("p t (i k) -> p i k t", k=TERMS)
+            k, factor = OPERANDS[first]
+            nc.gpsimd.tensor_scalar(
+                out=wq_tiles[group][:, first : first + count, rows, :].rearrange("p k i t -> p i k t"),
+                in0=by_feature[:, rows, k : k + count, :],
+                scalar1=factor, scalar2=0.0, op0=ALU.mult, op1=ALU.add,
+            )
+
+        def claim_wq(group):
+            wq = stage.tile([P, len(OPERANDS), P, PACK], BF16, tag="wq", align_bytes=64)
+            wq_tiles[group] = wq
 
         def multiply_wc(group, part):
-            count = part[1]
-            wq = wq_tiles[group, part]
+            first, count = part
+            wq = wq_tiles[group][:, first : first + count, :, :]
             nc.vector.tensor_tensor(
-                out=wq[:, 0:count, :, :],
-                in0=wq[:, 0:count, :, :],
+                out=wq, in0=wq,
                 in1=w_words[:, group * P : (group + 1) * P, :].unsqueeze(1).to_broadcast([P, count, P, PACK]),
                 op=ALU.mult,
             )
 
-        def multiply_first(part):
-            first, count = part
-            wq = stage.tile([P, 2, P, PACK], BF16, tag="wq", bufs=4, align_bytes=64)
+        def gather_weights(copy, w_rows, first, end):
+            copy(out=w_words[:, first:end, :], in_=w_rows[:].rearrange("p t i -> p i t"))
+
+        def multiply_first(place):
             by_plane = coeff_tiles[0][:].rearrange("p t (i k) -> p k i t", k=TERMS)
-            k, factor = OPERANDS[first]
+            k, factor = OPERANDS[place]
             nc.vector.scalar_tensor_tensor(
-                out=wq[:, 0, :, :], in0=by_plane[:, k, :, :], scalar=factor, in1=w_words[:, 0:P, :],
+                out=wq_tiles[0][:, place, :, :], in0=by_plane[:, k, :, :], scalar=factor, in1=w_words[:, 0:P, :],
                 op0=ALU.mult, op1=ALU.mult,
             )
-            wq_tiles[0, part] = wq
 
         def quantise_wc(group, part):
             first, count = part
             cols = slice(first * P, (first + count) * P)
-            flat = wq_tiles[group, part][:].rearrange("p k i t -> p (k i t)")
+            flat = wq_tiles[group][:].rearrange("p k i t -> p (k i t)")
             nc.vector.quantize_mx(
                 out=wc_codes[:, group, cols].bitcast(E4M3_X4),
                 scales=wc_scales[:, group, cols],
-                in_=flat[:, 0 : count * P * PACK],
-            )
-
-        def clamp_x(chunk):
-            blocks = slice(chunk * BLOCKS, (chunk + 1) * BLOCKS)
-            nc.vector.tensor_scalar(
-                out=x_rows[:, blocks, :], in0=x_rows[:, blocks, :],
-                scalar1=-X_LIMIT, scalar2=X_LIMIT, op0=ALU.max, op1=ALU.min,
+                in_=flat[:, first * P * PACK : (first + count) * P * PACK],
             )
 
         def turn_grad(chunk, half):
@@ -182,6 +190,13 @@ def tile_custombernsteinlayer_kernel(tc, x, weights, coeffs, grad_out, out):
                 )
             return x_t
 
+        def clamp_x(x_t):
+            x_held = stage.tile([P, CHUNK], BF16, tag="x_held", bufs=3)
+            nc.vector.tensor_scalar(
+                out=x_held[:], in0=x_t[:], scalar1=-X_LIMIT, scalar2=X_LIMIT, op0=ALU.max, op1=ALU.min
+            )
+            return x_held
+
         def scalar_planes(step, x_t):
             group, chunk = step
             e_low0 = stage.tile([P, CHUNK], F32, tag="e_low0")
@@ -208,10 +223,6 @@ def tile_custombernsteinlayer_kernel(tc, x, weights, coeffs, grad_out, out):
                 "e6": ("times", e_high[:, 1, :], -1.0),
                 "e7": ("times", e_high[:, 2, :], 1.0),
             }
-            exp_plane(e_low0[:], 0, binomial(ORDER - 1, 0))
-            exp_plane(e_low1[:], 1, binomial(ORDER - 1, 1))
-            for j in range(FLAT + 2, ORDER):
-                exp_plane(e_high[:, j - FLAT - 2, :], j, binomial(ORDER - 1, j))
             flat = binomial(ORDER - 1, FLAT)
             squares = []
             for side, line, square in ((-1, line_low, square_low), (1, line_high, square_high)):
@@ -224,16 +235,20 @@ def tile_custombernsteinlayer_kernel(tc, x, weights, coeffs, grad_out, out):
                 recipe["line_low" if side < 0 else "line_high"] = ("minus", line[:], gamma(k_near) * flat)
                 recipe["square_low" if side < 0 else "square_high"] = ("minus", square[:], gamma(k_far) * near * near / (4.0 * far))
                 squares.append((square, line, root / (gamma(k_near) * near), -root * middle))
-            nc.scalar.activation(out=t_part[:], in_=x_part, func=ACT.Tanh)
+            (low, low_line, low_scale, low_bias), (high, high_line, high_scale, high_bias) = squares
+            exp_plane(e_low0[:], 0, binomial(ORDER - 1, 0))
+            exp_plane(e_low1[:], 1, binomial(ORDER - 1, 1))
             exp_plane(line_low[:], FLAT - 1, gamma(FLAT) * binomial(ORDER - 1, FLAT - 1))
-            nc.scalar.activation(out=c_part[:], in_=t_part[:], func=ACT.Square)
+            nc.scalar.activation(out=t_part[:], in_=x_part, func=ACT.Tanh)
+            nc.scalar.activation(out=low[:], in_=low_line[:], func=ACT.Square, scale=low_scale, bias=low_bias)
             exp_plane(line_high[:], FLAT + 1, gamma(FLAT + 1) * binomial(ORDER - 1, FLAT + 1))
+            nc.scalar.activation(out=c_part[:], in_=t_part[:], func=ACT.Square)
+            nc.scalar.activation(out=high[:], in_=high_line[:], func=ACT.Square, scale=high_scale, bias=high_bias)
+            exp_plane(e_high[:, 0, :], FLAT + 2, binomial(ORDER - 1, FLAT + 2))
             nc.scalar.activation(out=c_part[:], in_=c_part[:], func=ACT.Square, scale=-1.0, bias=1.0)
-            for square, line, scale, bias in squares[:1]:
-                nc.scalar.activation(out=square[:], in_=line[:], func=ACT.Square, scale=scale, bias=bias)
+            exp_plane(e_high[:, 1, :], FLAT + 3, binomial(ORDER - 1, FLAT + 3))
+            exp_plane(e_high[:, 2, :], FLAT + 4, binomial(ORDER - 1, FLAT + 4))
             nc.scalar.activation(out=c_part[:], in_=c_part[:], func=ACT.Square)
-            for square, line, scale, bias in squares[1:]:
-                nc.scalar.activation(out=square[:], in_=line[:], func=ACT.Square, scale=scale, bias=bias)
             return {
                 "e_high": e_high, "d_six": d_six,
                 "recipe": recipe, "t": t_part, "c": c_part,
@@ -303,11 +318,12 @@ def tile_custombernsteinlayer_kernel(tc, x, weights, coeffs, grad_out, out):
         ctx.enter_context(tc.manual_schedule())
 
         load_x(0)
-        load_grad(0)
-        nc.sync.dma_start(out=w_rows[:], in_=weights.rearrange("(p t) i -> p t i", t=PACK))
+        load_weights(w_first, 0, P)
         load_coeffs(0)
+        load_grad(0)
         load_x(1)
         load_grad(1)
+        load_weights(w_later, P, FEATURES)
         load_x(2)
         load_coeffs(1)
         load_grad(2)
@@ -316,54 +332,58 @@ def tile_custombernsteinlayer_kernel(tc, x, weights, coeffs, grad_out, out):
 
         made = {}
         x_t = {}
-        clamp_x(0)
-        x_t[0] = turn_x(steps[0])
+        x_t[0] = clamp_x(turn_x(steps[0]))
         made[0] = scalar_planes(steps[0], x_t[0])
+        claim_wq(0)
+        gather_weights(nc.vector.tensor_copy, w_first, 0, P)
+        multiply_first(0)
+        multiply_first(1)
         for half in range(2):
             turn_grad(0, half)
+        x_t[1] = clamp_x(turn_x(steps[1]))
+        for block in ((2, 2, 0, P),) + pieces(*HIGH) + ((8, 1, 0, P),):
+            regroup(0, block)
+        difference(made[0])
+        quantise_wc(0, (0, 2))
         for half in range(2):
             gather_grad(0, half)
-        nc.vector.tensor_copy(out=w_words[:], in_=w_rows[:].rearrange("p t i -> p i t"))
+        multiply_wc(0, (2, 2))
         quantise_grad(0)
-        multiply_first(HEAD_PARTS[0])
-        multiply_first(HEAD_PARTS[1])
-        clamp_x(1)
-        x_t[1] = turn_x(steps[1])
-        regroup(0, HEAD_PARTS[2])
-        regroup(0, HEAD_PARTS[3])
-        difference(made[0])
-        regroup(0, HEAD_PARTS[4])
-        regroup(0, HEAD_PARTS[5])
-        quantise_wc(0, HEAD_PARTS[0])
-        quantise_wc(0, HEAD_PARTS[1])
-        head_multiply = {part[0] - 2: part for part in HEAD_PARTS[2:]}
-        head_quantise = {part[0] - 1: part for part in HEAD_PARTS[2:]}
+        quantise_wc(0, (2, 2))
+        head_parts = {2: (4, 4), 5: (8, 1)}
         slots = [(s, j) for s in range(last) for j in range(TERMS)]
         banks = {}
-        ready = 2
+        ready = 4
         products = {}
         totals = {}
         for n, (s, j) in enumerate(slots):
             group, chunk = steps[s]
-            parts = STEP_PARTS[chunk] if group + 1 < N_GROUPS else ()
+            preparing = group + 1 < N_GROUPS
             turning = group == 0 and chunk + 1 < N_CHUNKS
             if j == 0:
-                if chunk == 0 and group + 2 < N_GROUPS:
-                    load_coeffs(group + 2)
+                if chunk == 0:
+                    if group + 2 < N_GROUPS:
+                        load_coeffs(group + 2)
+                    if preparing:
+                        claim_wq(group + 1)
                 if s + 1 < last:
                     made[s + 1] = scalar_planes(steps[s + 1], x_t[s + 1])
-                for part in parts:
-                    regroup(group + 1, part)
-                if s + 1 < last:
-                    difference(made[s + 1])
+                if s == 0:
+                    gather_weights(nc.scalar.copy, w_later, P, FEATURES)
+                if s > 0:
+                    difference(made[s])
+                if preparing:
+                    for block in STEP_REGROUPS[chunk]:
+                        regroup(group + 1, block)
                 product_tile = stage.tile([P, TERMS, CHUNK], F32, tag="products")
                 products[s] = product_tile
-            if s == 0 and j in head_quantise:
-                quantise_wc(0, head_quantise[j])
-                quantised = sum(head_quantise[j])
-                ready = sum(1 for product in PRODUCTS if max(product[1]) < quantised)
-            if s == 0 and j in head_multiply:
-                multiply_wc(0, head_multiply[j])
+            if s == 0 and j in head_parts:
+                multiply_wc(0, head_parts[j])
+                quantise_wc(0, head_parts[j])
+                quantised = sum(head_parts[j])
+                ready = 0
+                while ready < TERMS and max(PRODUCTS[ready][1]) < quantised:
+                    ready += 1
             if n not in banks:
                 banks[n] = multiply(steps[s], j)
             weigh(banks[n], made[s], products[s], j)
@@ -374,29 +394,29 @@ def tile_custombernsteinlayer_kernel(tc, x, weights, coeffs, grad_out, out):
                 gather_grad(chunk + 1, j - 2)
             if turning and j == 4:
                 quantise_grad(chunk + 1)
-            if j == 6:
-                for part in parts:
+            if preparing and j == 6:
+                for part in STEP_PARTS[chunk]:
                     multiply_wc(group + 1, part)
             if (not turning and j >= 4) or j == 8 or (turning and j >= 5 and s > 0):
                 ready = TERMS * (s + 2)
             if j % RUN == RUN - 1 or s == 0:
-                for ahead in range(n + 1, min(n + 6, len(slots), ready)):
+                for ahead in range(n + 1, min(n + 7, len(slots), ready)):
                     if ahead not in banks:
                         ahead_s, ahead_j = slots[ahead]
                         banks[ahead] = multiply(steps[ahead_s], ahead_j)
             if turning and j in (0, 1):
                 turn_grad(chunk + 1, j)
+            if j == 2 and s + 2 < last:
+                turned_x = turn_x(steps[s + 2])
             if j == 5 and s + 2 < last:
-                if s + 2 < N_CHUNKS:
-                    clamp_x(s + 2)
-                x_t[s + 2] = turn_x(steps[s + 2])
+                x_t[s + 2] = clamp_x(turned_x)
             if j % RUN == RUN - 1:
                 if j == RUN - 1:
                     total = sum_psum.tile([P, BLOCKS, P], F32, tag="total")
                     totals[s] = total
                 add_up(totals[s], products[s], j + 1 - RUN, j + 1)
-            if j == TERMS - 1:
-                for part in parts:
+            if preparing and j == TERMS - 1:
+                for part in STEP_PARTS[chunk]:
                     quantise_wc(group + 1, part)
         scale_sum(made[last - 1], totals[last - 1])
         finish(steps[last - 1], made[last - 1])

@@ -106,16 +106,19 @@ def tile_custombernsteinlayer_kernel(tc, x, weights, coeffs, grad_out, out):
             nc.sync.dma_start(out=g_rows[:], in_=grad_out[rows, :].rearrange("(b p) o -> p b o", p=P))
             grad_tiles[chunk] = g_rows
 
-        def regroup(group, block):
+        def regroup(group, block, on_scalar=False):
             first, count, feature, features = block
             rows = slice(feature, feature + features)
             by_feature = coeff_tiles[group][:].rearrange("p t (i k) -> p i k t", k=TERMS)
             k, factor = OPERANDS[first]
-            nc.gpsimd.tensor_scalar(
-                out=wq_tiles[group][:, first : first + count, rows, :].rearrange("p k i t -> p i k t"),
-                in0=by_feature[:, rows, k : k + count, :],
-                scalar1=factor, scalar2=0.0, op0=ALU.mult, op1=ALU.add,
-            )
+            to = wq_tiles[group][:, first : first + count, rows, :].rearrange("p k i t -> p i k t")
+            source = by_feature[:, rows, k : k + count, :]
+            if on_scalar:
+                nc.scalar.activation(out=to, in_=source, func=ACT.Copy, scale=factor)
+            else:
+                nc.gpsimd.tensor_scalar(
+                    out=to, in0=source, scalar1=factor, scalar2=0.0, op0=ALU.mult, op1=ALU.add
+                )
 
         def claim_wq(group):
             wq = stage.tile([P, len(OPERANDS), P, PACK], BF16, tag="wq", align_bytes=64)
@@ -302,10 +305,10 @@ def tile_custombernsteinlayer_kernel(tc, x, weights, coeffs, grad_out, out):
             )
             made["scaled"] = scaled
 
-        def finish(step, made):
+        def finish(step, made, engine):
             group, chunk = step
             result = stage.tile([P, BLOCKS, P], F32, tag="result")
-            nc.gpsimd.tensor_tensor(out=result[:], in0=made["scaled"][:], in1=made["c"][:], op=ALU.mult)
+            engine.tensor_tensor(out=result[:], in0=made["scaled"][:], in1=made["c"][:], op=ALU.mult)
             nc.sync.dma_start(
                 out=out[chunk * CHUNK : (chunk + 1) * CHUNK, group * P : (group + 1) * P].rearrange(
                     "(b p) i -> p b i", p=P
@@ -341,8 +344,10 @@ def tile_custombernsteinlayer_kernel(tc, x, weights, coeffs, grad_out, out):
         for half in range(2):
             turn_grad(0, half)
         x_t[1] = clamp_x(turn_x(steps[1]))
-        for block in ((2, 2, 0, P),) + pieces(*HIGH) + ((8, 1, 0, P),):
+        for block in ((2, 2, 0, P),) + pieces(*HIGH):
             regroup(0, block)
+        for block in ((8, 1, 0, P),):
+            regroup(0, block, on_scalar=True)
         difference(made[0])
         quantise_wc(0, (0, 2))
         for half in range(2):
@@ -374,7 +379,7 @@ def tile_custombernsteinlayer_kernel(tc, x, weights, coeffs, grad_out, out):
                     difference(made[s])
                 if preparing:
                     for block in STEP_REGROUPS[chunk]:
-                        regroup(group + 1, block)
+                        regroup(group + 1, block, on_scalar=group == 0)
                 product_tile = stage.tile([P, TERMS, CHUNK], F32, tag="products")
                 products[s] = product_tile
             if s == 0 and j in head_parts:
@@ -389,7 +394,7 @@ def tile_custombernsteinlayer_kernel(tc, x, weights, coeffs, grad_out, out):
             weigh(banks[n], made[s], products[s], j)
             if j == 2 and s >= 1:
                 scale_sum(made[s - 1], totals[s - 1])
-                finish(steps[s - 1], made[s - 1])
+                finish(steps[s - 1], made[s - 1], nc.gpsimd)
             if turning and j in (2, 3):
                 gather_grad(chunk + 1, j - 2)
             if turning and j == 4:
@@ -419,4 +424,4 @@ def tile_custombernsteinlayer_kernel(tc, x, weights, coeffs, grad_out, out):
                 for part in STEP_PARTS[chunk]:
                     quantise_wc(group + 1, part)
         scale_sum(made[last - 1], totals[last - 1])
-        finish(steps[last - 1], made[last - 1])
+        finish(steps[last - 1], made[last - 1], nc.vector)

@@ -40,7 +40,7 @@ def pieces(first, count):
 
 
 STEP_REGROUPS = (((0, 1, 0, P),) + pieces(*LOW), pieces(*HIGH), ((8, 1, 0, P),), ())
-STEP_PARTS = (((0, 2),), ((2, 2),), ((4, 2),), ((6, 2), (8, 1)))
+STEP_PARTS = ((), ((0, 2),), ((2, 2), (4, 2)), ((6, 2), (8, 1)))
 
 FLOPS = 2 * TOKENS * OUTPUTS * FEATURES * TERMS
 
@@ -61,9 +61,9 @@ def tile_custombernsteinlayer_kernel(tc, x, weights, coeffs, grad_out, out):
     with ExitStack() as ctx:
         keep = ctx.enter_context(tc.tile_pool(name="keep", bufs=1))
         stage = ctx.enter_context(tc.tile_pool(name="stage", bufs=2))
-        mx_psum = ctx.enter_context(tc.psum_pool(name="mx_psum", bufs=6))
+        mx_psum = ctx.enter_context(tc.psum_pool(name="mx_psum", bufs=5))
         tr_psum = ctx.enter_context(tc.psum_pool(name="tr_psum", bufs=1))
-        sum_psum = ctx.enter_context(tc.psum_pool(name="sum_psum", bufs=1))
+        sum_psum = ctx.enter_context(tc.psum_pool(name="sum_psum", bufs=2))
 
         ident_f32 = keep.tile([P, P], F32)
         make_identity(nc, ident_f32[:])
@@ -392,20 +392,23 @@ def tile_custombernsteinlayer_kernel(tc, x, weights, coeffs, grad_out, out):
             if n not in banks:
                 banks[n] = multiply(steps[s], j)
             weigh(banks[n], made[s], products[s], j)
-            if j == 2 and s >= 1:
+            if preparing and j == 5:
+                for part in STEP_PARTS[chunk]:
+                    multiply_wc(group + 1, part)
+            if j == 6 and s >= 1:
                 scale_sum(made[s - 1], totals[s - 1])
                 finish(steps[s - 1], made[s - 1], nc.gpsimd)
+            if preparing and j == 6:
+                for part in STEP_PARTS[chunk]:
+                    quantise_wc(group + 1, part)
             if turning and j in (2, 3):
                 gather_grad(chunk + 1, j - 2)
             if turning and j == 4:
                 quantise_grad(chunk + 1)
-            if preparing and j == 6:
-                for part in STEP_PARTS[chunk]:
-                    multiply_wc(group + 1, part)
             if (not turning and j >= 4) or j == 8 or (turning and j >= 5 and s > 0):
                 ready = TERMS * (s + 2)
             if j % RUN == RUN - 1 or s == 0:
-                for ahead in range(n + 1, min(n + 7, len(slots), ready)):
+                for ahead in range(n + 1, min(n + 6, len(slots), ready)):
                     if ahead not in banks:
                         ahead_s, ahead_j = slots[ahead]
                         banks[ahead] = multiply(steps[ahead_s], ahead_j)
@@ -420,8 +423,5 @@ def tile_custombernsteinlayer_kernel(tc, x, weights, coeffs, grad_out, out):
                     total = sum_psum.tile([P, BLOCKS, P], F32, tag="total")
                     totals[s] = total
                 add_up(totals[s], products[s], j + 1 - RUN, j + 1)
-            if preparing and j == TERMS - 1:
-                for part in STEP_PARTS[chunk]:
-                    quantise_wc(group + 1, part)
         scale_sum(made[last - 1], totals[last - 1])
         finish(steps[last - 1], made[last - 1], nc.vector)

@@ -39,8 +39,8 @@ def pieces(first, count):
     return tuple((first, count, i * width, width) for i in range(PIECES))
 
 
-STEP_REGROUPS = (((0, 1, 0, P),) + pieces(*LOW), pieces(*HIGH), ((8, 1, 0, P),), ())
-STEP_PARTS = ((), ((0, 2),), ((2, 2), (4, 2)), ((6, 2), (8, 1)))
+STEP_REGROUPS = (((0, 1, 0, P),) + pieces(*LOW), pieces(*HIGH)[:1], pieces(*HIGH)[1:] + ((8, 1, 0, P),), ())
+STEP_PARTS = ((), ((0, 4),), (), ((4, 4), (8, 1)))
 
 FLOPS = 2 * TOKENS * OUTPUTS * FEATURES * TERMS
 
@@ -200,6 +200,13 @@ def tile_custombernsteinlayer_kernel(tc, x, weights, coeffs, grad_out, out):
             )
             return x_held
 
+        def squares_late(step):
+            group, chunk = step
+            return group == N_GROUPS - 1 or (chunk >= 2 and group > 0)
+
+        def last_square(made):
+            nc.gpsimd.tensor_tensor(out=made["c"][:], in0=made["c"][:], in1=made["c"][:], op=ALU.mult)
+
         def scalar_planes(step, x_t):
             group, chunk = step
             e_low0 = stage.tile([P, CHUNK], F32, tag="e_low0")
@@ -251,7 +258,8 @@ def tile_custombernsteinlayer_kernel(tc, x, weights, coeffs, grad_out, out):
             nc.scalar.activation(out=c_part[:], in_=c_part[:], func=ACT.Square, scale=-1.0, bias=1.0)
             exp_plane(e_high[:, 1, :], FLAT + 3, binomial(ORDER - 1, FLAT + 3))
             exp_plane(e_high[:, 2, :], FLAT + 4, binomial(ORDER - 1, FLAT + 4))
-            nc.scalar.activation(out=c_part[:], in_=c_part[:], func=ACT.Square)
+            if not squares_late(step):
+                nc.scalar.activation(out=c_part[:], in_=c_part[:], func=ACT.Square)
             return {
                 "e_high": e_high, "d_six": d_six,
                 "recipe": recipe, "t": t_part, "c": c_part,
@@ -377,9 +385,11 @@ def tile_custombernsteinlayer_kernel(tc, x, weights, coeffs, grad_out, out):
                     gather_weights(nc.scalar.copy, w_later, P, FEATURES)
                 if s > 0:
                     difference(made[s])
+                if squares_late(steps[s]):
+                    last_square(made[s])
                 if preparing:
                     for block in STEP_REGROUPS[chunk]:
-                        regroup(group + 1, block, on_scalar=group == 0)
+                        regroup(group + 1, block, on_scalar=group == 0 or block[1] == 1)
                 product_tile = stage.tile([P, TERMS, CHUNK], F32, tag="products")
                 products[s] = product_tile
             if s == 0 and j in head_parts:

import math
from contextlib import ExitStack

import concourse.mybir as mybir
from concourse.masks import make_identity

F32 = mybir.dt.float32
BF16 = mybir.dt.bfloat16
U32 = mybir.dt.uint32
U8 = mybir.dt.uint8
E4M3_X4 = mybir.dt.float8_e4m3fn_x4
E5M2_X4 = mybir.dt.float8_e5m2_x4
ALU = mybir.AluOpType
ACT = mybir.ActivationFunctionType

P = 128
PACK = 4
TOKENS, FEATURES, OUTPUTS, ORDER = 2048, 512, 512, 8
TERMS = ORDER + 1
CHUNK = 512
BLOCKS = CHUNK // P
N_CHUNKS = TOKENS // CHUNK
N_GROUPS = FEATURES // P
FLAT = 3
RUN = 3
X_LIMIT = 8.0
OPERANDS = ((0, 8.0), (1, -1.0), (2, -1.0), (3, -1.0), (4, 1.0), (5, 1.0), (6, 1.0), (7, 1.0), (8, -8.0))
PRODUCTS = (
    ("e0", (0, 1)), ("e1", (1,)), ("line_low", (3,)),
    ("square_low", (2,)), ("line_high", (4,)), ("square_high", (5,)),
    ("e6", (7,)), ("e7", (7, 8)), ("d6", (6,)),
)
LOW, HIGH = (1, 3), (4, 4)
PIECES = 2


def pieces(first, count):
    width = P // PIECES
    return tuple((first, count, i * width, width) for i in range(PIECES))


STEP_REGROUPS = (((0, 1, 0, P),) + pieces(*LOW), pieces(*HIGH)[:1], pieces(*HIGH)[1:] + ((8, 1, 0, P),), ())
STEP_PARTS = ((), ((0, 4),), (), ((4, 4), (8, 1)))

FLOPS = 2 * TOKENS * OUTPUTS * FEATURES * TERMS


def binomial(n, k):
    value = 1
    for j in range(k):
        value = value * (n - j) // (j + 1)
    return value


def gamma(k):
    return 8.0 / binomial(ORDER, k)


def tile_custombernsteinlayer_kernel(tc, x, weights, coeffs, grad_out, out):
    nc = tc.nc
    with ExitStack() as ctx:
        keep = ctx.enter_context(tc.tile_pool(name="keep", bufs=1))
        stage = ctx.enter_context(tc.tile_pool(name="stage", bufs=2))
        mx_psum = ctx.enter_context(tc.psum_pool(name="mx_psum", bufs=5))
        tr_psum = ctx.enter_context(tc.psum_pool(name="tr_psum", bufs=1))
        sum_psum = ctx.enter_context(tc.psum_pool(name="sum_psum", bufs=2))

        ident_f32 = keep.tile([P, P], F32)
        make_identity(nc, ident_f32[:])
        ident_bf16 = keep.tile([P, P], BF16)
        make_identity(nc, ident_bf16[:])

        x_rows = keep.tile([P, N_CHUNKS * BLOCKS, FEATURES], BF16)
        w_first = keep.tile([P, PACK, P], BF16)
        w_later = keep.tile([P, PACK, FEATURES - P], BF16)
        w_words = keep.tile([P, FEATURES, PACK], BF16)
        g_codes = keep.tile([P, TOKENS], U32, align_bytes=64)
        g_scales = keep.tile([P, TOKENS], U8, align_bytes=64)
        wc_codes = keep.tile([P, N_GROUPS, TERMS * P], U32, align_bytes=64)
        wc_scales = keep.tile([P, N_GROUPS, TERMS * P], U8, align_bytes=64)

        coeff_view = coeffs.rearrange("(p t) i k -> p t (i k)", t=PACK)
        group_cols = P * TERMS
        coeff_tiles = {}
        grad_tiles = {}
        gq_tiles = {}
        wq_tiles = {}
        turned = {}

        def load_coeffs(group):
            co = stage.tile([P, PACK, group_cols], BF16, tag="co")
            nc.sync.dma_start(out=co[:], in_=coeff_view[:, :, group * group_cols : (group + 1) * group_cols])
            coeff_tiles[group] = co

        def load_weights(w_rows, first, end):
            nc.sync.dma_start(out=w_rows[:], in_=weights.rearrange("(p t) i -> p t i", t=PACK)[:, :, first:end])

        def load_x(chunk):
            rows = slice(chunk * CHUNK, (chunk + 1) * CHUNK)
            blocks = slice(chunk * BLOCKS, (chunk + 1) * BLOCKS)
            nc.sync.dma_start(out=x_rows[:, blocks, :], in_=x[rows, :].rearrange("(b p) i -> p b i", p=P))

        def load_grad(chunk):
            rows = slice(chunk * CHUNK, (chunk + 1) * CHUNK)
            g_rows = stage.tile([P, BLOCKS, OUTPUTS], BF16, tag="g_rows", bufs=4)
            nc.sync.dma_start(out=g_rows[:], in_=grad_out[rows, :].rearrange("(b p) o -> p b o", p=P))
            grad_tiles[chunk] = g_rows

        def regroup(group, block, on_scalar=False):
            first, count, feature, features = block
            rows = slice(feature, feature + features)
            by_feature = coeff_tiles[group][:].rearrange("p t (i k) -> p i k t", k=TERMS)
            k, factor = OPERANDS[first]
            to = wq_tiles[group][:, first : first + count, rows, :].rearrange("p k i t -> p i k t")
            source = by_feature[:, rows, k : k + count, :]
            if on_scalar:
                nc.scalar.activation(out=to, in_=source, func=ACT.Copy, scale=factor)
            else:
                nc.gpsimd.tensor_scalar(
                    out=to, in0=source, scalar1=factor, scalar2=0.0, op0=ALU.mult, op1=ALU.add
                )

        def claim_wq(group):
            wq = stage.tile([P, len(OPERANDS), P, PACK], BF16, tag="wq", align_bytes=64)
            wq_tiles[group] = wq

        def multiply_wc(group, part):
            first, count = part
            wq = wq_tiles[group][:, first : first + count, :, :]
            nc.vector.tensor_tensor(
                out=wq, in0=wq,
                in1=w_words[:, group * P : (group + 1) * P, :].unsqueeze(1).to_broadcast([P, count, P, PACK]),
                op=ALU.mult,
            )

        def gather_weights(copy, w_rows, first, end):
            copy(out=w_words[:, first:end, :], in_=w_rows[:].rearrange("p t i -> p i t"))

        def multiply_first(place):
            by_plane = coeff_tiles[0][:].rearrange("p t (i k) -> p k i t", k=TERMS)
            k, factor = OPERANDS[place]
            nc.vector.scalar_tensor_tensor(
                out=wq_tiles[0][:, place, :, :], in0=by_plane[:, k, :, :], scalar=factor, in1=w_words[:, 0:P, :],
                op0=ALU.mult, op1=ALU.mult,
            )

        def quantise_wc(group, part):
            first, count = part
            cols = slice(first * P, (first + count) * P)
            flat = wq_tiles[group][:].rearrange("p k i t -> p (k i t)")
            nc.vector.quantize_mx(
                out=wc_codes[:, group, cols].bitcast(E4M3_X4),
                scales=wc_scales[:, group, cols],
                in_=flat[:, first * P * PACK : (first + count) * P * PACK],
            )

        def turn_grad(chunk, half):
            g_words = grad_tiles[chunk][:].bitcast(F32)
            g_t = mx_psum.tile([P, 2, 2 * P], F32, tag="g_k")
            for b in range(2):
                for u in range(2):
                    nc.tensor.transpose(
                        out=g_t[:, u, b * P : (b + 1) * P],
                        in_=g_words[:, 2 * half + b, u : 2 * P : 2],
                        identity=ident_f32[:],
                    )
            turned[chunk, half] = g_t

        def gather_grad(chunk, half):
            if half == 0:
                gq = stage.tile([P, CHUNK * PACK], BF16, tag="gq", align_bytes=64)
                gq_tiles[chunk] = gq
            gq_words = gq_tiles[chunk][:].bitcast(F32).rearrange("p (n u) -> p n u", u=2)
            nc.vector.tensor_copy(
                out=gq_words[:, half * 2 * P : (half + 1) * 2 * P, :],
                in_=turned[chunk, half][:].rearrange("p u n -> p n u"),
            )

        def quantise_grad(chunk):
            cols = slice(chunk * CHUNK, (chunk + 1) * CHUNK)
            nc.vector.quantize_mx(
                out=g_codes[:, cols].bitcast(E5M2_X4), scales=g_scales[:, cols], in_=gq_tiles[chunk][:]
            )

        def turn_x(step):
            group, chunk = step
            x_t = tr_psum.tile([P, CHUNK], BF16, tag="tr")
            for b in range(BLOCKS):
                nc.tensor.transpose(
                    out=x_t[:, b * P : (b + 1) * P],
                    in_=x_rows[:, chunk * BLOCKS + b, group * P : (group + 1) * P],
                    identity=ident_bf16[:],
                )
            return x_t

        def clamp_x(x_t):
            x_held = stage.tile([P, CHUNK], BF16, tag="x_held", bufs=3)
            nc.vector.tensor_scalar(
                out=x_held[:], in0=x_t[:], scalar1=-X_LIMIT, scalar2=X_LIMIT, op0=ALU.max, op1=ALU.min
            )
            return x_held

        def squares_late(step):
            group, chunk = step
            return group == N_GROUPS - 1 or (chunk >= 2 and group > 0)

        def last_square(made):
            nc.gpsimd.tensor_tensor(out=made["c"][:], in0=made["c"][:], in1=made["c"][:], op=ALU.mult)

        def scalar_planes(step, x_t):
            group, chunk = step
            e_low0 = stage.tile([P, CHUNK], F32, tag="e_low0")
            e_low1 = stage.tile([P, CHUNK], F32, tag="e_low1")
            e_high = stage.tile([P, 3, CHUNK], F32, tag="e_high")
            line_low = stage.tile([P, CHUNK], F32, tag="line_low")
            line_high = stage.tile([P, CHUNK], F32, tag="line_high")
            square_low = stage.tile([P, CHUNK], F32, tag="square_low")
            square_high = stage.tile([P, CHUNK], F32, tag="square_high")
            d_six = stage.tile([P, CHUNK], F32, tag="d_six")
            t_part = stage.tile([P, BLOCKS, P], F32, tag="t_part", bufs=3)
            c_part = stage.tile([P, BLOCKS, P], F32, tag="c_part", bufs=3)
            x_part = x_rows[:, chunk * BLOCKS : (chunk + 1) * BLOCKS, group * P : (group + 1) * P]

            def exp_plane(out_plane, j, gain):
                nc.scalar.activation(
                    out=out_plane, in_=x_t[:], func=ACT.Exp, scale=float(2 * (j - FLAT)), bias=math.log(gain)
                )

            recipe = {
                "e0": ("times", e_low0[:], 1.0),
                "e1": ("times", e_low1[:], -1.0),
                "d6": ("times", d_six[:], -gamma(ORDER - 2)),
                "e6": ("times", e_high[:, 1, :], -1.0),
                "e7": ("times", e_high[:, 2, :], 1.0),
            }
            flat = binomial(ORDER - 1, FLAT)
            squares = []
            for side, line, square in ((-1, line_low, square_low), (1, line_high, square_high)):
                near = binomial(ORDER - 1, FLAT + side)
                far = binomial(ORDER - 1, FLAT + 2 * side)
                k_near = FLAT if side < 0 else FLAT + 1
                k_far = k_near + side
                middle = near / (2.0 * far)
                root = math.sqrt(gamma(k_far) * far)
                recipe["line_low" if side < 0 else "line_high"] = ("minus", line[:], gamma(k_near) * flat)
                recipe["square_low" if side < 0 else "square_high"] = ("minus", square[:], gamma(k_far) * near * near / (4.0 * far))
                squares.append((square, line, root / (gamma(k_near) * near), -root * middle))
            (low, low_line, low_scale, low_bias), (high, high_line, high_scale, high_bias) = squares
            exp_plane(e_low0[:], 0, binomial(ORDER - 1, 0))
            exp_plane(e_low1[:], 1, binomial(ORDER - 1, 1))
            exp_plane(line_low[:], FLAT - 1, gamma(FLAT) * binomial(ORDER - 1, FLAT - 1))
            nc.scalar.activation(out=t_part[:], in_=x_part, func=ACT.Tanh)
            nc.scalar.activation(out=low[:], in_=low_line[:], func=ACT.Square, scale=low_scale, bias=low_bias)
            exp_plane(line_high[:], FLAT + 1, gamma(FLAT + 1) * binomial(ORDER - 1, FLAT + 1))
            nc.scalar.activation(out=c_part[:], in_=t_part[:], func=ACT.Square)
            nc.scalar.activation(out=high[:], in_=high_line[:], func=ACT.Square, scale=high_scale, bias=high_bias)
            exp_plane(e_high[:, 0, :], FLAT + 2, binomial(ORDER - 1, FLAT + 2))
            nc.scalar.activation(out=c_part[:], in_=c_part[:], func=ACT.Square, scale=-1.0, bias=1.0)
            exp_plane(e_high[:, 1, :], FLAT + 3, binomial(ORDER - 1, FLAT + 3))
            exp_plane(e_high[:, 2, :], FLAT + 4, binomial(ORDER - 1, FLAT + 4))
            if not squares_late(step):
                nc.scalar.activation(out=c_part[:], in_=c_part[:], func=ACT.Square)
            return {
                "e_high": e_high, "d_six": d_six,
                "recipe": recipe, "t": t_part, "c": c_part,
            }

        def difference(made):
            nc.gpsimd.tensor_tensor(
                out=made["d_six"][:], in0=made["e_high"][:, 0, :], in1=made["e_high"][:, 1, :], op=ALU.subtract
            )

        def multiply(step, j):
            group, chunk = step
            cols = slice(chunk * CHUNK, (chunk + 1) * CHUNK)
            g_k = mx_psum.tile([P, CHUNK], F32, tag="g_k")
            places = PRODUCTS[j][1]
            for i, place in enumerate(places):
                nc.tensor.matmul_mx(
                    out=g_k[:],
                    lhsT=wc_codes[:, group, place * P : (place + 1) * P].bitcast(E4M3_X4),
                    lhsT_scale=wc_scales[:, group, place * P : (place + 1) * P],
                    rhs=g_codes[:, cols].bitcast(E5M2_X4),
                    rhs_scale=g_scales[:, cols],
                    start=(i == 0),
                    stop=(i == len(places) - 1),
                )
            return g_k

        def weigh(g_k, made, products, j):
            form, plane, number = made["recipe"][PRODUCTS[j][0]]
            nc.vector.scalar_tensor_tensor(
                out=products[:, j, :], in0=plane, scalar=number, in1=g_k[:],
                op0=ALU.mult if form == "times" else ALU.subtract, op1=ALU.mult,
            )

        def add_up(total, products, first, last):
            for j in range(first, last):
                for b in range(BLOCKS):
                    nc.tensor.matmul(
                        out=total[:, b, :],
                        lhsT=products[:, j, b * P : (b + 1) * P],
                        rhs=ident_f32[:],
                        is_transpose=True,
                        start=(j == 0 and b == 0),
                        stop=(j == TERMS - 1 and b == BLOCKS - 1),
                    )

        def scale_sum(made, total):
            scaled = stage.tile([P, BLOCKS, P], F32, tag="scaled")
            nc.vector.scalar_tensor_tensor(
                out=scaled[:], in0=made["t"][:], scalar=1.0, in1=total[:], op0=ALU.subtract, op1=ALU.mult
            )
            made["scaled"] = scaled

        def finish(step, made, engine):
            group, chunk = step
            result = stage.tile([P, BLOCKS, P], F32, tag="result")
            engine.tensor_tensor(out=result[:], in0=made["scaled"][:], in1=made["c"][:], op=ALU.mult)
            nc.sync.dma_start(
                out=out[chunk * CHUNK : (chunk + 1) * CHUNK, group * P : (group + 1) * P].rearrange(
                    "(b p) i -> p b i", p=P
                ),
                in_=result[:],
            )

        steps = [(group, chunk) for group in range(N_GROUPS) for chunk in range(N_CHUNKS)]
        last = len(steps)
        ctx.enter_context(tc.manual_schedule())

        load_x(0)
        load_weights(w_first, 0, P)
        load_coeffs(0)
        load_grad(0)
        load_x(1)
        load_grad(1)
        load_weights(w_later, P, FEATURES)
        load_x(2)
        load_coeffs(1)
        load_grad(2)
        load_x(3)
        load_grad(3)

        made = {}
        x_t = {}
        x_t[0] = clamp_x(turn_x(steps[0]))
        made[0] = scalar_planes(steps[0], x_t[0])
        claim_wq(0)
        gather_weights(nc.vector.tensor_copy, w_first, 0, P)
        multiply_first(0)
        multiply_first(1)
        for half in range(2):
            turn_grad(0, half)
        x_t[1] = clamp_x(turn_x(steps[1]))
        for block in ((2, 2, 0, P),) + pieces(*HIGH):
            regroup(0, block)
        for block in ((8, 1, 0, P),):
            regroup(0, block, on_scalar=True)
        difference(made[0])
        quantise_wc(0, (0, 2))
        for half in range(2):
            gather_grad(0, half)
        multiply_wc(0, (2, 2))
        quantise_grad(0)
        quantise_wc(0, (2, 2))
        head_parts = {2: (4, 4), 5: (8, 1)}
        slots = [(s, j) for s in range(last) for j in range(TERMS)]
        banks = {}
        ready = 4
        products = {}
        totals = {}
        for n, (s, j) in enumerate(slots):
            group, chunk = steps[s]
            preparing = group + 1 < N_GROUPS
            turning = group == 0 and chunk + 1 < N_CHUNKS
            if j == 0:
                if chunk == 0:
                    if group + 2 < N_GROUPS:
                        load_coeffs(group + 2)
                    if preparing:
                        claim_wq(group + 1)
                if s + 1 < last:
                    made[s + 1] = scalar_planes(steps[s + 1], x_t[s + 1])
                if s == 0:
                    gather_weights(nc.scalar.copy, w_later, P, FEATURES)
                if s > 0:
                    difference(made[s])
                if squares_late(steps[s]):
                    last_square(made[s])
                if preparing:
                    for block in STEP_REGROUPS[chunk]:
                        regroup(group + 1, block, on_scalar=group == 0 or block[1] == 1)
                product_tile = stage.tile([P, TERMS, CHUNK], F32, tag="products")
                products[s] = product_tile
            if s == 0 and j in head_parts:
                multiply_wc(0, head_parts[j])
                quantise_wc(0, head_parts[j])
                quantised = sum(head_parts[j])
                ready = 0
                while ready < TERMS and max(PRODUCTS[ready][1]) < quantised:
                    ready += 1
            if n not in banks:
                banks[n] = multiply(steps[s], j)
            weigh(banks[n], made[s], products[s], j)
            if preparing and j == 5:
                for part in STEP_PARTS[chunk]:
                    multiply_wc(group + 1, part)
            if j == 6 and s >= 1:
                scale_sum(made[s - 1], totals[s - 1])
                finish(steps[s - 1], made[s - 1], nc.gpsimd)
            if preparing and j == 6:
                for part in STEP_PARTS[chunk]:
                    quantise_wc(group + 1, part)
            if turning and j in (2, 3):
                gather_grad(chunk + 1, j - 2)
            if turning and j == 4:
                quantise_grad(chunk + 1)
            if (not turning and j >= 4) or j == 8 or (turning and j >= 5 and s > 0):
                ready = TERMS * (s + 2)
            if j % RUN == RUN - 1 or s == 0:
                for ahead in range(n + 1, min(n + 6, len(slots), ready)):
                    if ahead not in banks:
                        ahead_s, ahead_j = slots[ahead]
                        banks[ahead] = multiply(steps[ahead_s], ahead_j)
            if turning and j in (0, 1):
                turn_grad(chunk + 1, j)
            if j == 2 and s + 2 < last:
                turned_x = turn_x(steps[s + 2])
            if j == 5 and s + 2 < last:
                x_t[s + 2] = clamp_x(turned_x)
            if j % RUN == RUN - 1:
                if j == RUN - 1:
                    total = sum_psum.tile([P, BLOCKS, P], F32, tag="total")
                    totals[s] = total
                add_up(totals[s], products[s], j + 1 - RUN, j + 1)
        scale_sum(made[last - 1], totals[last - 1])
        finish(steps[last - 1], made[last - 1], nc.vector)
